import numpy as np
import ml_dtypes


def mxq(x, axis, fmt="e4m3"):
    dtype, down = {"e4m3": (ml_dtypes.float8_e4m3fn, 7), "e5m2": (ml_dtypes.float8_e5m2, 14)}[fmt]
    v = np.moveaxis(np.asarray(x, np.float32).astype(ml_dtypes.bfloat16).astype(np.float64), axis, -1)
    blocks = v.reshape(v.shape[:-1] + (-1, 32))
    amax = np.abs(blocks).max(-1, keepdims=True)
    byte = np.maximum(np.where(amax > 0, np.frexp(amax)[1] - 1 + 127, 0) - down, 1)
    scale = np.exp2(byte - 127.0)
    codes = (blocks / scale).astype(np.float32).astype(dtype).astype(np.float64)
    return np.moveaxis((codes * scale).reshape(v.shape), -1, axis)


WIDE = False


def mx_kscale(k):
    if not WIDE:
        return np.ones(k)
    levels = np.array([10, -10, 5, -5, 0])
    a = np.random.permutation(np.resize(levels, k // 512 * 4)).reshape(k // 512, 4)
    idx = np.arange(k)
    return np.exp2(a[idx // 512, idx % 128 // 32])


BF16 = ml_dtypes.bfloat16


def bf(x):
    return np.asarray(x, np.float32).astype(BF16)


def f64(x):
    return np.asarray(x).astype(np.float64)


B, I, O = 16384, 64, 128
GRID_SIZE = 5
SPLINE_ORDER = 3
NUM_BASIS = GRID_SIZE + SPLINE_ORDER
K = I * NUM_BASIS
GRID = np.linspace(-1.0, 1.0, GRID_SIZE + 2 * SPLINE_ORDER + 1)
EPS = 1e-6
X0 = 0.5 * np.log(2.0 / (GRID[1] - GRID[0]))


def bspline_basis(x):
    xe = x[..., None]
    bas = ((xe >= GRID[:-1]) & (xe < GRID[1:])).astype(np.float64)
    for k in range(1, SPLINE_ORDER + 1):
        nb = bas.shape[-1] - 1
        g_i = GRID[:nb]
        g_i1 = GRID[1:1 + nb]
        g_ik = GRID[k:k + nb]
        g_ik1 = GRID[k + 1:k + 1 + nb]
        dl = g_ik - g_i
        dr = g_ik1 - g_i1
        left = np.where(dl > EPS, (xe - g_i) / np.where(dl > EPS, dl, 1.0), 0.0) * bas[..., :nb]
        right = np.where(dr > EPS, (g_ik1 - xe) / np.where(dr > EPS, dr, 1.0), 0.0) * bas[..., 1:nb + 1]
        bas = left + right
    return bas[..., :NUM_BASIS]


def setup_inputs():
    a = np.log2(mx_kscale(K))[::NUM_BASIS]
    n = np.random.standard_normal((B, I))
    tail = -np.sign(a) * (X0 + np.abs(a) * np.log(2.0) / 3.0) + 0.15 * n
    c = np.exp2(2.0 * np.abs(a))
    return {"x": bf(np.where(a == 0, n, tail)),
            "spline_coeffs": bf(np.random.standard_normal((O, I, NUM_BASIS)) * (2.0 / np.sqrt(I)) * c[None, :, None])}


def reference(x, spline_coeffs):
    xn = np.tanh(f64(x))
    basis = bspline_basis(xn)
    bq = mxq(basis.reshape(B, K), 1, "e4m3")
    wq = mxq(f64(spline_coeffs).reshape(O, K), 1, "e4m3")
    return bq @ wq.T

@@ -1,0 +1,132 @@
+from contextlib import ExitStack
+
+import concourse.mybir as mybir
+from concourse.masks import make_identity
+
+FLOPS = 2 * 16384 * 512 * 128
+
+F32 = mybir.dt.float32
+BF16 = mybir.dt.bfloat16
+U32 = mybir.dt.uint32
+U8 = mybir.dt.uint8
+FP8X4 = mybir.dt.float8_e4m3fn_x4
+ALU = mybir.AluOpType
+AF = mybir.ActivationFunctionType
+
+P = 128
+ROWS = 128
+FEAT = 64
+OUTS = 128
+RC = 8
+C = RC * P
+NCH = ROWS // RC
+
+
+def tile_kan_layer_t_kernel(tc, x, spline_coeffs, out):
+    nc = tc.nc
+    x_v = x.rearrange("(p r) i -> p r i", r=ROWS)
+    out_v = out.rearrange("(p r) o -> p r o", r=ROWS)
+    with ExitStack() as ctx:
+        const = ctx.enter_context(tc.tile_pool(name="const", bufs=1))
+        work = ctx.enter_context(tc.tile_pool(name="work", bufs=2))
+        big = ctx.enter_context(tc.tile_pool(name="big", bufs=2))
+        outp = ctx.enter_context(tc.tile_pool(name="outp", bufs=3))
+        ps_t = ctx.enter_context(tc.psum_pool(name="ps_t", bufs=2))
+        ps_o = ctx.enter_context(tc.psum_pool(name="ps_o", bufs=3))
+        ps_w = ctx.enter_context(tc.psum_pool(name="ps_w", bufs=1))
+
+        x_sb = const.tile([P, ROWS, FEAT], BF16)
+        w_sb = const.tile([P, FEAT * 8], BF16)
+        nc.sync.dma_start(out=x_sb[:, 0:8, :], in_=x_v[:, 0:8, :])
+        nc.sync.dma_start(out=w_sb[:], in_=spline_coeffs.rearrange("o i k -> o (i k)"))
+        nc.sync.dma_start(out=x_sb[:, 8:32, :], in_=x_v[:, 8:32, :])
+        nc.sync.dma_start(out=x_sb[:, 32:64, :], in_=x_v[:, 32:64, :])
+        nc.sync.dma_start(out=x_sb[:, 64:128, :], in_=x_v[:, 64:128, :])
+
+        ident = const.tile([P, P], BF16)
+        make_identity(nc, ident[:])
+        par = const.tile([P, 1], F32)
+        nc.vector.tensor_reduce(
+            out=par[:],
+            in_=ident[:].rearrange("p (a two) -> p a two", two=2)[:, :, 1],
+            axis=mybir.AxisListType.X,
+            op=ALU.add,
+        )
+        sc = const.tile([P, 1], F32)
+        nc.vector.tensor_scalar(out=sc[:], in0=par[:], scalar1=-4.0, scalar2=2.0, op0=ALU.mult, op1=ALU.add)
+        nb = const.tile([P, 4], F32)
+        for t in range(4):
+            nc.vector.memset(nb[:, t : t + 1], -(t + 2.0))
+
+        w3 = w_sb[:].rearrange("o (i k) -> o i k", k=8)
+        wg = const.tile([P, 4, FEAT, 2], BF16)
+        for t in range(4):
+            nc.vector.tensor_copy(out=wg[:, t, :, 0], in_=w3[:, :, t])
+            nc.vector.tensor_copy(out=wg[:, t, :, 1], in_=w3[:, :, 7 - t])
+        w_t = ps_w.tile([P, 4, OUTS], BF16)
+        for t in range(4):
+            nc.tensor.transpose(w_t[:, t, :], wg[:, t, :, :].rearrange("o i h -> o (i h)"), ident[:])
+        wq = const.tile([P, OUTS, 4], BF16, align_bytes=64)
+        nc.vector.tensor_copy(out=wq[:], in_=w_t[:].rearrange("p t o -> p o t"))
+        w_codes = const.tile([P, OUTS], U32, align_bytes=64)
+        w_scales = const.tile([P, OUTS], U8, align_bytes=64)
+        nc.vector.quantize_mx(
+            out=w_codes[:].bitcast(FP8X4), scales=w_scales[:], in_=wq[:].rearrange("p o t -> p (o t)")
+        )
+
+        for ch in range(NCH):
+            r0 = ch * RC
+            xd = work.tile([P, RC, FEAT, 2], BF16)
+            nc.vector.tensor_copy(
+                out=xd[:], in_=x_sb[:, r0 : r0 + RC, :].unsqueeze(3).to_broadcast([P, RC, FEAT, 2])
+            )
+            x_t = ps_t.tile([P, C], BF16)
+            for j in range(RC):
+                nc.tensor.transpose(
+                    x_t[:, j * P : (j + 1) * P], xd[:, j, :, :].rearrange("p i h -> p (i h)"), ident[:]
+                )
+            sg = work.tile([P, C], F32)
+            nc.scalar.activation(out=sg[:], in_=x_t[:], func=AF.Sigmoid, scale=sc[:, 0:1])
+
+            rt = big.tile([P, 4, C], F32)
+            qt = big.tile([P, 4, C], F32)
+            et = big.tile([P, 4, C], F32)
+            for t in range(4):
+                nc.scalar.activation(out=rt[:, t, :], in_=sg[:], func=AF.Abs, bias=nb[:, t : t + 1], scale=11.0)
+                nc.scalar.activation(out=qt[:, t, :], in_=sg[:], func=AF.Square, bias=nb[:, t : t + 1], scale=11.0)
+            nc.vector.tensor_scalar(out=rt[:], in0=rt[:], scalar1=2.0, scalar2=0.0, op0=ALU.subtract, op1=ALU.min)
+            nc.scalar.activation(out=et[:], in_=rt[:], func=AF.Square)
+            nc.vector.scalar_tensor_tensor(out=qt[:], in0=rt[:], scalar=0.5, in1=qt[:], op0=ALU.mult, op1=ALU.mult)
+            nc.vector.scalar_tensor_tensor(
+                out=et[:], in0=rt[:], scalar=-1.0 / 6.0, in1=et[:], op0=ALU.mult, op1=ALU.mult
+            )
+            g = work.tile([P, C, 4], BF16, align_bytes=64)
+            nc.vector.scalar_tensor_tensor(
+                out=g[:],
+                in0=qt[:].rearrange("p t c -> p c t"),
+                scalar=2.0 / 3.0,
+                in1=et[:].rearrange("p t c -> p c t"),
+                op0=ALU.add,
+                op1=ALU.min,
+            )
+            codes = work.tile([P, C], U32, align_bytes=64)
+            scales = work.tile([P, C], U8, align_bytes=64)
+            nc.vector.quantize_mx(
+                out=codes[:].bitcast(FP8X4), scales=scales[:], in_=g[:].rearrange("p c t -> p (c t)")
+            )
+            osb = outp.tile([P, RC, OUTS], F32)
+            for q in range(RC // 4):
+                acc = ps_o.tile([P, 4, OUTS], F32)
+                for j in range(4):
+                    c0 = (q * 4 + j) * P
+                    nc.tensor.matmul_mx(
+                        out=acc[:, j, :],
+                        lhsT=codes[:, c0 : c0 + P].bitcast(FP8X4),
+                        lhsT_scale=scales[:, c0 : c0 + P],
+                        rhs=w_codes[:].bitcast(FP8X4),
+                        rhs_scale=w_scales[:],
+                        start=True,
+                        stop=True,
+                    )
+                nc.scalar.copy(out=osb[:, q * 4 : q * 4 + 4, :], in_=acc[:])
+            nc.sync.dma_start(out=out_v[:, r0 : r0 + RC, :], in_=osb[:])

@@ -17,9 +17,9 @@ P = 128
 ROWS = 128
 FEAT = 64
 OUTS = 128
-RC = 8
-C = RC * P
-NCH = ROWS // RC
+CHUNKS = ((2,0),(2,64),(4,192),(8,384),(8,384),(8,384),(8,384),(8,384),(8,384),(8,384),(8,384),(8,384),(8,384),(8,384),(8,384),(8,384),(8,384),(4,256),(2,160),(2,256))
+LOADS = ((0,2),(2,8),(8,32),(32,64),(64,128))
+assert sum(c[0] for c in CHUNKS) == ROWS
 
 
 def tile_kan_layer_t_kernel(tc, x, spline_coeffs, out):
@@ -28,8 +28,8 @@ def tile_kan_layer_t_kernel(tc, x, spline_coeffs, out):
     out_v = out.rearrange("(p r) o -> p r o", r=ROWS)
     with ExitStack() as ctx:
         const = ctx.enter_context(tc.tile_pool(name="const", bufs=1))
-        work = ctx.enter_context(tc.tile_pool(name="work", bufs=2))
-        big = ctx.enter_context(tc.tile_pool(name="big", bufs=2))
+        actp = ctx.enter_context(tc.tile_pool(name="actp", bufs=3))
+        dvep = ctx.enter_context(tc.tile_pool(name="dvep", bufs=2))
         outp = ctx.enter_context(tc.tile_pool(name="outp", bufs=3))
         ps_t = ctx.enter_context(tc.psum_pool(name="ps_t", bufs=2))
         ps_o = ctx.enter_context(tc.psum_pool(name="ps_o", bufs=3))
@@ -37,11 +37,10 @@ def tile_kan_layer_t_kernel(tc, x, spline_coeffs, out):
 
         x_sb = const.tile([P, ROWS, FEAT], BF16)
         w_sb = const.tile([P, FEAT * 8], BF16)
-        nc.sync.dma_start(out=x_sb[:, 0:8, :], in_=x_v[:, 0:8, :])
-        nc.sync.dma_start(out=w_sb[:], in_=spline_coeffs.rearrange("o i k -> o (i k)"))
-        nc.sync.dma_start(out=x_sb[:, 8:32, :], in_=x_v[:, 8:32, :])
-        nc.sync.dma_start(out=x_sb[:, 32:64, :], in_=x_v[:, 32:64, :])
-        nc.sync.dma_start(out=x_sb[:, 64:128, :], in_=x_v[:, 64:128, :])
+        for n, (a, b) in enumerate(LOADS):
+            nc.sync.dma_start(out=x_sb[:, a:b, :], in_=x_v[:, a:b, :])
+            if n == 0:
+                nc.sync.dma_start(out=w_sb[:], in_=spline_coeffs.rearrange("o i k -> o (i k)"))
 
         ident = const.tile([P, P], BF16)
         make_identity(nc, ident[:])
@@ -54,71 +53,95 @@ def tile_kan_layer_t_kernel(tc, x, spline_coeffs, out):
         )
         sc = const.tile([P, 1], F32)
         nc.vector.tensor_scalar(out=sc[:], in0=par[:], scalar1=-4.0, scalar2=2.0, op0=ALU.mult, op1=ALU.add)
-        nb = const.tile([P, 4], F32)
-        for t in range(4):
-            nc.vector.memset(nb[:, t : t + 1], -(t + 2.0))
+        nb = const.tile([P, 5], F32)
+        for col, val in enumerate((-6.0, -8.0, -4.0, -2.0, -0.5)):
+            nc.vector.memset(nb[:, col : col + 1], val)
 
-        w3 = w_sb[:].rearrange("o (i k) -> o i k", k=8)
-        wg = const.tile([P, 4, FEAT, 2], BF16)
-        for t in range(4):
-            nc.vector.tensor_copy(out=wg[:, t, :, 0], in_=w3[:, :, t])
-            nc.vector.tensor_copy(out=wg[:, t, :, 1], in_=w3[:, :, 7 - t])
-        w_t = ps_w.tile([P, 4, OUTS], BF16)
-        for t in range(4):
-            nc.tensor.transpose(w_t[:, t, :], wg[:, t, :, :].rearrange("o i h -> o (i h)"), ident[:])
-        wq = const.tile([P, OUTS, 4], BF16, align_bytes=64)
-        nc.vector.tensor_copy(out=wq[:], in_=w_t[:].rearrange("p t o -> p o t"))
         w_codes = const.tile([P, OUTS], U32, align_bytes=64)
         w_scales = const.tile([P, OUTS], U8, align_bytes=64)
-        nc.vector.quantize_mx(
-            out=w_codes[:].bitcast(FP8X4), scales=w_scales[:], in_=wq[:].rearrange("p o t -> p (o t)")
-        )
 
-        for ch in range(NCH):
-            r0 = ch * RC
-            xd = work.tile([P, RC, FEAT, 2], BF16)
-            nc.vector.tensor_copy(
-                out=xd[:], in_=x_sb[:, r0 : r0 + RC, :].unsqueeze(3).to_broadcast([P, RC, FEAT, 2])
+        def weights():
+            w3 = w_sb[:].rearrange("o (i k) -> o i k", k=8)
+            wg = const.tile([P, 4, FEAT, 2], BF16)
+            for t in range(4):
+                nc.vector.tensor_copy(out=wg[:, t, :, 0], in_=w3[:, :, 2 * t])
+                nc.vector.tensor_copy(out=wg[:, t, :, 1], in_=w3[:, :, 7 - 2 * t])
+            w_t = ps_w.tile([P, 4, OUTS], BF16)
+            for t in range(4):
+                nc.tensor.transpose(w_t[:, t, :], wg[:, t, :, :].rearrange("o i h -> o (i h)"), ident[:])
+            wq = const.tile([P, OUTS, 4], BF16, align_bytes=64)
+            nc.vector.tensor_copy(out=wq[:], in_=w_t[:].rearrange("p t o -> p o t"))
+            nc.vector.quantize_mx(
+                out=w_codes[:].bitcast(FP8X4), scales=w_scales[:], in_=wq[:].rearrange("p o t -> p (o t)")
             )
-            x_t = ps_t.tile([P, C], BF16)
-            for j in range(RC):
+
+        def front(r0, rc):
+            c = rc * P
+            xd = dvep.tile([P, rc, FEAT, 2], BF16, name="xd")
+            nc.vector.tensor_copy(
+                out=xd[:], in_=x_sb[:, r0 : r0 + rc, :].unsqueeze(3).to_broadcast([P, rc, FEAT, 2])
+            )
+            x_t = ps_t.tile([P, c], BF16, name="x_t")
+            for j in range(rc):
                 nc.tensor.transpose(
                     x_t[:, j * P : (j + 1) * P], xd[:, j, :, :].rearrange("p i h -> p (i h)"), ident[:]
                 )
-            sg = work.tile([P, C], F32)
+            sg = actp.tile([P, c], F32, name="sg")
             nc.scalar.activation(out=sg[:], in_=x_t[:], func=AF.Sigmoid, scale=sc[:, 0:1])
+            uv1 = actp.tile([P, 2, c], F32, name="uv1")
+            nc.scalar.activation(out=uv1[:, 0, :], in_=sg[:], func=AF.Abs, bias=nb[:, 0:1], scale=11.0)
+            nc.scalar.activation(out=uv1[:, 1, :], in_=sg[:], func=AF.Abs, bias=nb[:, 1:2], scale=11.0)
+            uv2 = actp.tile([P, 2, c], F32, name="uv2")
+            nc.scalar.activation(out=uv2[:], in_=uv1[:], func=AF.Abs, bias=nb[:, 2:3])
+            ee = actp.tile([P, c], F32, name="ee")
+            nc.scalar.activation(out=ee[:], in_=uv2[:, 0, :], func=AF.Abs, bias=nb[:, 3:4])
+            cc = actp.tile([P, c], F32, name="cc")
+            nc.scalar.activation(out=cc[:], in_=ee[:], func=AF.Square, bias=nb[:, 4:5], scale=0.5)
+            ss = actp.tile([P, 2, c], F32, name="ss")
+            nc.scalar.activation(out=ss[:], in_=uv2[:], func=AF.Square, bias=nb[:, 4:5], scale=0.25)
+            return sg, uv1, uv2, ee, cc, ss
 
-            rt = big.tile([P, 4, C], F32)
-            qt = big.tile([P, 4, C], F32)
-            et = big.tile([P, 4, C], F32)
-            for t in range(4):
-                nc.scalar.activation(out=rt[:, t, :], in_=sg[:], func=AF.Abs, bias=nb[:, t : t + 1], scale=11.0)
-                nc.scalar.activation(out=qt[:, t, :], in_=sg[:], func=AF.Square, bias=nb[:, t : t + 1], scale=11.0)
-            nc.vector.tensor_scalar(out=rt[:], in0=rt[:], scalar1=2.0, scalar2=0.0, op0=ALU.subtract, op1=ALU.min)
-            nc.scalar.activation(out=et[:], in_=rt[:], func=AF.Square)
-            nc.vector.scalar_tensor_tensor(out=qt[:], in0=rt[:], scalar=0.5, in1=qt[:], op0=ALU.mult, op1=ALU.mult)
+        def middle(rc, acols, tiles):
+            c = rc * P
+            sg, uv1, uv2, ee, cc, ss = tiles
+            nc.vector.scalar_tensor_tensor(out=cc[:], in0=ee[:], scalar=1.0, in1=cc[:], op0=ALU.subtract, op1=ALU.mult)
+            qn = dvep.tile([P, 2, c], F32, name="qn")
             nc.vector.scalar_tensor_tensor(
-                out=et[:], in0=rt[:], scalar=-1.0 / 6.0, in1=et[:], op0=ALU.mult, op1=ALU.mult
+                out=qn[:, 0, :], in0=sg[:], scalar=8.0 / 11.0, in1=cc[:], op0=ALU.is_gt, op1=ALU.add
             )
-            g = work.tile([P, C, 4], BF16, align_bytes=64)
             nc.vector.scalar_tensor_tensor(
-                out=g[:],
-                in0=qt[:].rearrange("p t c -> p c t"),
-                scalar=2.0 / 3.0,
-                in1=et[:].rearrange("p t c -> p c t"),
-                op0=ALU.add,
-                op1=ALU.min,
+                out=qn[:, 1, :], in0=uv1[:, 0, :], scalar=4.0, in1=cc[:], op0=ALU.is_gt, op1=ALU.subtract
             )
-            codes = work.tile([P, C], U32, align_bytes=64)
-            scales = work.tile([P, C], U8, align_bytes=64)
+            nc.vector.scalar_tensor_tensor(out=ss[:], in0=uv2[:], scalar=2.0, in1=ss[:], op0=ALU.subtract, op1=ALU.mult)
+            zz = dvep.tile([P, 4, c], F32, name="zz")
+            nc.vector.scalar_tensor_tensor(out=zz[:, 0:2, :], in0=qn[:], scalar=0.0, in1=ss[:], op0=ALU.max, op1=ALU.add)
+            nc.vector.scalar_tensor_tensor(
+                out=zz[:, 2:4, :], in0=qn[:], scalar=0.0, in1=ss[:], op0=ALU.max, op1=ALU.subtract
+            )
+            g = dvep.tile([P, c, 4], BF16, align_bytes=64, name="g")
+            zp = zz[:].rearrange("p t c -> p c t")
+            dc = c - acols
+            if dc:
+                nc.vector.tensor_scalar(
+                    out=g[:, 0:dc, :], in0=zp[:, 0:dc, :], scalar1=-8.0 / 3.0, scalar2=0.0, op0=ALU.mult, op1=ALU.max
+                )
+            if acols:
+                nc.scalar.activation(out=g[:, dc:c, :], in_=zp[:, dc:c, :], func=AF.Relu, scale=-8.0 / 3.0)
+            return g
+
+        def back(r0, rc, g):
+            c = rc * P
+            codes = dvep.tile([P, c], U32, align_bytes=64, name="codes")
+            scales = dvep.tile([P, c], U8, align_bytes=64, name="scales")
             nc.vector.quantize_mx(
                 out=codes[:].bitcast(FP8X4), scales=scales[:], in_=g[:].rearrange("p c t -> p (c t)")
             )
-            osb = outp.tile([P, RC, OUTS], F32)
-            for q in range(RC // 4):
-                acc = ps_o.tile([P, 4, OUTS], F32)
-                for j in range(4):
-                    c0 = (q * 4 + j) * P
+            osb = outp.tile([P, rc, OUTS], F32, name="osb")
+            for q0 in range(0, rc, 4):
+                n = min(4, rc - q0)
+                acc = ps_o.tile([P, n, OUTS], F32, name="acc")
+                for j in range(n):
+                    c0 = (q0 + j) * P
                     nc.tensor.matmul_mx(
                         out=acc[:, j, :],
                         lhsT=codes[:, c0 : c0 + P].bitcast(FP8X4),
@@ -128,5 +151,17 @@ def tile_kan_layer_t_kernel(tc, x, spline_coeffs, out):
                         start=True,
                         stop=True,
                     )
-                nc.scalar.copy(out=osb[:, q * 4 : q * 4 + 4, :], in_=acc[:])
-            nc.sync.dma_start(out=out_v[:, r0 : r0 + RC, :], in_=osb[:])
+                nc.scalar.copy(out=osb[:, q0 : q0 + n, :], in_=acc[:])
+            nc.sync.dma_start(out=out_v[:, r0 : r0 + rc, :], in_=osb[:])
+
+        starts = []
+        r0 = 0
+        for rc, acols in CHUNKS:
+            starts.append(r0)
+            r0 += rc
+        for n, (rc, acols) in enumerate(CHUNKS):
+            tiles = front(starts[n], rc)
+            if n == 0:
+                weights()
+            g = middle(rc, acols, tiles)
+            back(starts[n], rc, g)

@@ -47,8 +47,8 @@ def tile_kan_layer_t_kernel(tc, x, spline_coeffs, out):
         par = const.tile([P, 1], F32)
         nc.vector.tensor_reduce(
             out=par[:],
-            in_=ident[:].rearrange("p (a two) -> p a two", two=2)[:, :, 1],
-            axis=mybir.AxisListType.X,
+            in_=ident[:].rearrange("p (a h j) -> p a h j", h=2, j=4)[:, :, 1, :],
+            axis=mybir.AxisListType.XY,
             op=ALU.add,
         )
         sc = const.tile([P, 1], F32)
@@ -61,14 +61,14 @@ def tile_kan_layer_t_kernel(tc, x, spline_coeffs, out):
         w_scales = const.tile([P, OUTS], U8, align_bytes=64)
 
         def weights():
-            w3 = w_sb[:].rearrange("o (i k) -> o i k", k=8)
-            wg = const.tile([P, 4, FEAT, 2], BF16)
+            w4 = w_sb[:].rearrange("o (a j k) -> o a j k", j=4, k=8)
+            wg = const.tile([P, 4, FEAT // 4, 2, 4], BF16)
             for t in range(4):
-                nc.vector.tensor_copy(out=wg[:, t, :, 0], in_=w3[:, :, 2 * t])
-                nc.vector.tensor_copy(out=wg[:, t, :, 1], in_=w3[:, :, 7 - 2 * t])
+                nc.vector.tensor_copy(out=wg[:, t, :, 0, :], in_=w4[:, :, :, 2 * t])
+                nc.vector.tensor_copy(out=wg[:, t, :, 1, :], in_=w4[:, :, :, 7 - 2 * t])
             w_t = ps_w.tile([P, 4, OUTS], BF16)
             for t in range(4):
-                nc.tensor.transpose(w_t[:, t, :], wg[:, t, :, :].rearrange("o i h -> o (i h)"), ident[:])
+                nc.tensor.transpose(w_t[:, t, :], wg[:, t, :, :, :].rearrange("o a h j -> o (a h j)"), ident[:])
             wq = const.tile([P, OUTS, 4], BF16, align_bytes=64)
             nc.vector.tensor_copy(out=wq[:], in_=w_t[:].rearrange("p t o -> p o t"))
             nc.vector.quantize_mx(
@@ -77,14 +77,19 @@ def tile_kan_layer_t_kernel(tc, x, spline_coeffs, out):
 
         def front(r0, rc):
             c = rc * P
-            xd = dvep.tile([P, rc, FEAT, 2], BF16, name="xd")
+            xd = dvep.tile([P, rc * (FEAT // 4), 2, 4], BF16, name="xd")
             nc.vector.tensor_copy(
-                out=xd[:], in_=x_sb[:, r0 : r0 + rc, :].unsqueeze(3).to_broadcast([P, rc, FEAT, 2])
+                out=xd[:],
+                in_=x_sb[:, r0 : r0 + rc, :]
+                .rearrange("p r (a j) -> p (r a) j", j=4)
+                .unsqueeze(2)
+                .to_broadcast([P, rc * (FEAT // 4), 2, 4]),
             )
+            xf = xd[:].rearrange("p n h j -> p (n h j)")
             x_t = ps_t.tile([P, c], BF16, name="x_t")
             for j in range(rc):
                 nc.tensor.transpose(
-                    x_t[:, j * P : (j + 1) * P], xd[:, j, :, :].rearrange("p i h -> p (i h)"), ident[:]
+                    x_t[:, j * P : (j + 1) * P], xf[:, j * P : (j + 1) * P], ident[:]
                 )
             sg = actp.tile([P, c], F32, name="sg")
             nc.scalar.activation(out=sg[:], in_=x_t[:], func=AF.Sigmoid, scale=sc[:, 0:1])
@@ -119,14 +124,23 @@ def tile_kan_layer_t_kernel(tc, x, spline_coeffs, out):
                 out=zz[:, 2:4, :], in0=qn[:], scalar=0.0, in1=ss[:], op0=ALU.max, op1=ALU.subtract
             )
             g = dvep.tile([P, c, 4], BF16, align_bytes=64, name="g")
-            zp = zz[:].rearrange("p t c -> p c t")
             dc = c - acols
             if dc:
                 nc.vector.tensor_scalar(
-                    out=g[:, 0:dc, :], in0=zp[:, 0:dc, :], scalar1=-8.0 / 3.0, scalar2=0.0, op0=ALU.mult, op1=ALU.max
+                    out=g[:, 0:dc, :].rearrange("p (c i) t -> p c t i", i=4),
+                    in0=zz[:, :, 0:dc].rearrange("p t (c i) -> p c t i", i=4),
+                    scalar1=-8.0 / 3.0,
+                    scalar2=0.0,
+                    op0=ALU.mult,
+                    op1=ALU.max,
                 )
             if acols:
-                nc.scalar.activation(out=g[:, dc:c, :], in_=zp[:, dc:c, :], func=AF.Relu, scale=-8.0 / 3.0)
+                nc.scalar.activation(
+                    out=g[:, dc:c, :].rearrange("p (c i) t -> p c t i", i=4),
+                    in_=zz[:, :, dc:c].rearrange("p t (c i) -> p c t i", i=4),
+                    func=AF.Relu,
+                    scale=-8.0 / 3.0,
+                )
             return g
 
         def back(r0, rc, g):

@@ -17,9 +17,10 @@ P = 128
 ROWS = 128
 FEAT = 64
 OUTS = 128
-CHUNKS = ((2,0),(2,64),(4,192),(8,384),(8,384),(8,384),(8,384),(8,384),(8,384),(8,384),(8,384),(8,384),(8,384),(8,384),(8,384),(8,384),(8,384),(4,256),(2,160),(2,256))
-LOADS = ((0,2),(2,8),(8,32),(32,64),(64,128))
-assert sum(c[0] for c in CHUNKS) == ROWS
+CHUNKS = (2, 2, 4) + (8,) * 14 + (4, 2, 2)
+LOADS = ((0, 2), (2, 8), (8, 32), (32, 64), (64, 128))
+SLOT_K = (4, 6, 0, 2)
+assert sum(CHUNKS) == ROWS
 
 
 def tile_kan_layer_t_kernel(tc, x, spline_coeffs, out):
@@ -28,12 +29,13 @@ def tile_kan_layer_t_kernel(tc, x, spline_coeffs, out):
     out_v = out.rearrange("(p r) o -> p r o", r=ROWS)
     with ExitStack() as ctx:
         const = ctx.enter_context(tc.tile_pool(name="const", bufs=1))
-        actp = ctx.enter_context(tc.tile_pool(name="actp", bufs=3))
+        fold = ctx.enter_context(tc.tile_pool(name="fold", bufs=2))
+        actp = ctx.enter_context(tc.tile_pool(name="actp", bufs=2))
         dvep = ctx.enter_context(tc.tile_pool(name="dvep", bufs=2))
         outp = ctx.enter_context(tc.tile_pool(name="outp", bufs=3))
-        ps_t = ctx.enter_context(tc.psum_pool(name="ps_t", bufs=2))
-        ps_o = ctx.enter_context(tc.psum_pool(name="ps_o", bufs=3))
-        ps_w = ctx.enter_context(tc.psum_pool(name="ps_w", bufs=1))
+        ps_t = ctx.enter_context(tc.psum_pool(name="ps_t", bufs=4))
+        ps_u = ctx.enter_context(tc.psum_pool(name="ps_u", bufs=2))
+        ps_o = ctx.enter_context(tc.psum_pool(name="ps_o", bufs=2))
 
         x_sb = const.tile([P, ROWS, FEAT], BF16)
         w_sb = const.tile([P, FEAT * 8], BF16)
@@ -42,20 +44,16 @@ def tile_kan_layer_t_kernel(tc, x, spline_coeffs, out):
             if n == 0:
                 nc.sync.dma_start(out=w_sb[:], in_=spline_coeffs.rearrange("o i k -> o (i k)"))
 
-        ident = const.tile([P, P], BF16)
+        ident = const.tile([P, P], F32)
         make_identity(nc, ident[:])
-        par = const.tile([P, 1], F32)
-        nc.vector.tensor_reduce(
-            out=par[:],
-            in_=ident[:].rearrange("p (a h j) -> p a h j", h=2, j=4)[:, :, 1, :],
-            axis=mybir.AxisListType.XY,
-            op=ALU.add,
-        )
-        sc = const.tile([P, 1], F32)
-        nc.vector.tensor_scalar(out=sc[:], in0=par[:], scalar1=-4.0, scalar2=2.0, op0=ALU.mult, op1=ALU.add)
-        nb = const.tile([P, 5], F32)
-        for col, val in enumerate((-6.0, -8.0, -4.0, -2.0, -0.5)):
-            nc.vector.memset(nb[:, col : col + 1], val)
+        ident_b = const.tile([P, P], BF16)
+        nc.vector.tensor_copy(out=ident_b[:], in_=ident[:])
+        one = const.tile([P, 1], F32)
+        nc.vector.memset(one[:], 1.0)
+        neg = const.tile([P, 1], F32)
+        nc.vector.memset(neg[:], -1.0)
+        two_thirds = const.tile([P, 1], F32)
+        nc.vector.tensor_scalar(out=two_thirds[:], in0=one[:], scalar1=2.0 / 3.0, scalar2=None, op0=ALU.mult)
 
         w_codes = const.tile([P, OUTS], U32, align_bytes=64)
         w_scales = const.tile([P, OUTS], U8, align_bytes=64)
@@ -64,83 +62,92 @@ def tile_kan_layer_t_kernel(tc, x, spline_coeffs, out):
             w4 = w_sb[:].rearrange("o (a j k) -> o a j k", j=4, k=8)
             wg = const.tile([P, 4, FEAT // 4, 2, 4], BF16)
             for t in range(4):
-                nc.vector.tensor_copy(out=wg[:, t, :, 0, :], in_=w4[:, :, :, 2 * t])
-                nc.vector.tensor_copy(out=wg[:, t, :, 1, :], in_=w4[:, :, :, 7 - 2 * t])
-            w_t = ps_w.tile([P, 4, OUTS], BF16)
+                nc.vector.tensor_copy(out=wg[:, t, :, 0, :], in_=w4[:, :, :, SLOT_K[t]])
+                nc.vector.tensor_copy(out=wg[:, t, :, 1, :], in_=w4[:, :, :, 7 - SLOT_K[t]])
+            w_t = ps_o.tile([P, 4, OUTS], BF16, name="acc")
             for t in range(4):
-                nc.tensor.transpose(w_t[:, t, :], wg[:, t, :, :, :].rearrange("o a h j -> o (a h j)"), ident[:])
+                nc.tensor.transpose(w_t[:, t, :], wg[:, t, :, :, :].rearrange("o a h j -> o (a h j)"), ident_b[:])
             wq = const.tile([P, OUTS, 4], BF16, align_bytes=64)
             nc.vector.tensor_copy(out=wq[:], in_=w_t[:].rearrange("p t o -> p o t"))
             nc.vector.quantize_mx(
                 out=w_codes[:].bitcast(FP8X4), scales=w_scales[:], in_=wq[:].rearrange("p o t -> p (o t)")
             )
 
-        def front(r0, rc):
-            c = rc * P
-            xd = dvep.tile([P, rc * (FEAT // 4), 2, 4], BF16, name="xd")
-            nc.vector.tensor_copy(
-                out=xd[:],
-                in_=x_sb[:, r0 : r0 + rc, :]
-                .rearrange("p r (a j) -> p (r a) j", j=4)
-                .unsqueeze(2)
-                .to_broadcast([P, rc * (FEAT // 4), 2, 4]),
-            )
-            xf = xd[:].rearrange("p n h j -> p (n h j)")
-            x_t = ps_t.tile([P, c], BF16, name="x_t")
-            for j in range(rc):
-                nc.tensor.transpose(
-                    x_t[:, j * P : (j + 1) * P], xf[:, j * P : (j + 1) * P], ident[:]
-                )
-            sg = actp.tile([P, c], F32, name="sg")
-            nc.scalar.activation(out=sg[:], in_=x_t[:], func=AF.Sigmoid, scale=sc[:, 0:1])
-            uv1 = actp.tile([P, 2, c], F32, name="uv1")
-            nc.scalar.activation(out=uv1[:, 0, :], in_=sg[:], func=AF.Abs, bias=nb[:, 0:1], scale=11.0)
-            nc.scalar.activation(out=uv1[:, 1, :], in_=sg[:], func=AF.Abs, bias=nb[:, 1:2], scale=11.0)
-            uv2 = actp.tile([P, 2, c], F32, name="uv2")
-            nc.scalar.activation(out=uv2[:], in_=uv1[:], func=AF.Abs, bias=nb[:, 2:3])
-            ee = actp.tile([P, c], F32, name="ee")
-            nc.scalar.activation(out=ee[:], in_=uv2[:, 0, :], func=AF.Abs, bias=nb[:, 3:4])
-            cc = actp.tile([P, c], F32, name="cc")
-            nc.scalar.activation(out=cc[:], in_=ee[:], func=AF.Square, bias=nb[:, 4:5], scale=0.5)
-            ss = actp.tile([P, 2, c], F32, name="ss")
-            nc.scalar.activation(out=ss[:], in_=uv2[:], func=AF.Square, bias=nb[:, 4:5], scale=0.25)
-            return sg, uv1, uv2, ee, cc, ss
+        def folds(r0, rc):
+            sg = fold.tile([P, rc, FEAT // 4, 2, 4], F32, name="sg")
+            xin = x_sb[:, r0 : r0 + rc, :].rearrange("p r (a j) -> p r a j", j=4)
+            for h in range(2):
+                nc.scalar.activation(out=sg[:, :, :, h, :], in_=xin, func=AF.Sigmoid, scale=2.0 - 4.0 * h)
+            s = sg[:].rearrange("p r a h j -> p (r a h j)")
+            m = fold.tile([P, rc * P], F32, name="m")
+            nc.vector.tensor_scalar(out=m[:], in0=s, scalar1=-0.5, scalar2=-3.0 / 11, op0=ALU.mult, op1=ALU.add)
+            ca = fold.tile([P, rc * P], F32, name="ca")
+            nc.vector.tensor_scalar(out=ca[:], in0=s, scalar1=2.0 / 11, scalar2=6.0 / 11, op0=ALU.max, op1=ALU.min)
+            cb = fold.tile([P, rc * P], F32, name="cb")
+            nc.vector.tensor_scalar(out=cb[:], in0=s, scalar1=4.0 / 11, scalar2=8.0 / 11, op0=ALU.max, op1=ALU.min)
+            na = fold.tile([P, rc * P], F32, name="na")
+            nc.vector.tensor_scalar(out=na[:], in0=m[:], scalar1=1.0 / 11, scalar2=-6.0 / 11, op0=ALU.add, op1=ALU.max)
+            nb = fold.tile([P, rc * P], F32, name="nb")
+            nc.vector.tensor_scalar(out=nb[:], in0=m[:], scalar1=-8.0 / 11, scalar2=-4.0 / 11, op0=ALU.max, op1=ALU.min)
+            return m, ca, cb, na, nb
 
-        def middle(rc, acols, tiles):
+        def add_t(dst, one_plane, other_plane, r):
+            for n, plane in enumerate((one_plane, other_plane)):
+                nc.tensor.matmul(
+                    dst, lhsT=plane[:, r * P : (r + 1) * P], rhs=ident[:], start=n == 0, stop=n == 1, is_transpose=True
+                )
+
+        def cubes(rc, planes):
+            m, ca, cb, na, nb = planes
             c = rc * P
-            sg, uv1, uv2, ee, cc, ss = tiles
-            nc.vector.scalar_tensor_tensor(out=cc[:], in0=ee[:], scalar=1.0, in1=cc[:], op0=ALU.subtract, op1=ALU.mult)
-            qn = dvep.tile([P, 2, c], F32, name="qn")
-            nc.vector.scalar_tensor_tensor(
-                out=qn[:, 0, :], in0=sg[:], scalar=8.0 / 11.0, in1=cc[:], op0=ALU.is_gt, op1=ALU.add
-            )
-            nc.vector.scalar_tensor_tensor(
-                out=qn[:, 1, :], in0=uv1[:, 0, :], scalar=4.0, in1=cc[:], op0=ALU.is_gt, op1=ALU.subtract
-            )
-            nc.vector.scalar_tensor_tensor(out=ss[:], in0=uv2[:], scalar=2.0, in1=ss[:], op0=ALU.subtract, op1=ALU.mult)
-            zz = dvep.tile([P, 4, c], F32, name="zz")
-            nc.vector.scalar_tensor_tensor(out=zz[:, 0:2, :], in0=qn[:], scalar=0.0, in1=ss[:], op0=ALU.max, op1=ALU.add)
-            nc.vector.scalar_tensor_tensor(
-                out=zz[:, 2:4, :], in0=qn[:], scalar=0.0, in1=ss[:], op0=ALU.max, op1=ALU.subtract
-            )
-            g = dvep.tile([P, c, 4], BF16, align_bytes=64, name="g")
-            dc = c - acols
-            if dc:
-                nc.vector.tensor_scalar(
-                    out=g[:, 0:dc, :].rearrange("p (c i) t -> p c t i", i=4),
-                    in0=zz[:, :, 0:dc].rearrange("p t (c i) -> p c t i", i=4),
-                    scalar1=-8.0 / 3.0,
-                    scalar2=0.0,
-                    op0=ALU.mult,
-                    op1=ALU.max,
-                )
-            if acols:
+            t2 = actp.tile([P, c, 2], F32, name="t2")
+            t3 = dvep.tile([P, c, 2], BF16, name="t3")
+            ee = actp.tile([P, c], F32, name="ee")
+            for q0 in range(0, rc, 4):
+                n = min(4, rc - q0)
+                uu = ps_u.tile([P, n, P], F32, name="uu")
+                for r in range(n):
+                    add_t(uu[:, r, :], cb, m, q0 + r)
                 nc.scalar.activation(
-                    out=g[:, dc:c, :].rearrange("p (c i) t -> p c t i", i=4),
-                    in_=zz[:, :, dc:c].rearrange("p t (c i) -> p c t i", i=4),
-                    func=AF.Relu,
-                    scale=-8.0 / 3.0,
+                    out=ee[:, q0 * P : (q0 + n) * P], in_=uu[:].rearrange("p r c -> p (r c)"), func=AF.Abs, scale=22.0
                 )
+                for p0 in range(q0, q0 + n, 2):
+                    tt = ps_t.tile([P, 2, 2, P], F32, name="tt")
+                    for r in range(2):
+                        add_t(tt[:, 0, r, :], ca, na, p0 + r)
+                        add_t(tt[:, 1, r, :], cb, nb, p0 + r)
+                    tv = tt[:].rearrange("p s r c -> p (r c) s")
+                    cols = slice(p0 * P, (p0 + 2) * P)
+                    nc.scalar.activation(
+                        out=t2[:, cols, :], in_=tv, func=AF.Square, scale=(22.0**3 / 6.0) ** 0.5
+                    )
+                    nc.vector.tensor_tensor(out=t3[:, cols, :], in0=tv, in1=t2[:, cols, :], op=ALU.mult)
+            yy = actp.tile([P, c], F32, name="yy")
+            nc.scalar.activation(out=yy[:], in_=ee[:], func=AF.Abs, bias=neg[:, 0:1])
+            vv = actp.tile([P, c], F32, name="vv")
+            nc.scalar.activation(out=vv[:], in_=yy[:], func=AF.Square, bias=one[:, 0:1], scale=-1.0)
+            return t3, yy, vv
+
+        def values(rc, tiles):
+            t3, yy, vv = tiles
+            c = rc * P
+            nc.vector.scalar_tensor_tensor(out=vv[:], in0=yy[:], scalar=1.0, in1=vv[:], op0=ALU.add, op1=ALU.mult)
+            gd = actp.tile([P, c, 2], BF16, name="gd")
+            nc.scalar.activation(
+                out=gd[:], in_=vv[:].unsqueeze(2).to_broadcast([P, c, 2]), func=AF.Identity, bias=two_thirds[:, 0:1], scale=-0.5
+            )
+            pp = dvep.tile([P, 2, c, 2], BF16, name="pp")
+            for s in range(2):
+                nc.vector.tensor_scalar(
+                    out=pp[:, s, :, :], in0=t3[:], scalar1=1.0 - 2.0 * s, scalar2=0.0, op0=ALU.mult, op1=ALU.max
+                )
+            g = dvep.tile([P, c, 2, 2], BF16, align_bytes=64, name="g")
+            nc.vector.tensor_tensor(
+                out=g[:],
+                in0=pp[:].rearrange("p s c f -> p c s f"),
+                in1=gd[:].unsqueeze(2).to_broadcast([P, c, 2, 2]),
+                op=ALU.min,
+            )
             return g
 
         def back(r0, rc, g):
@@ -148,7 +155,7 @@ def tile_kan_layer_t_kernel(tc, x, spline_coeffs, out):
             codes = dvep.tile([P, c], U32, align_bytes=64, name="codes")
             scales = dvep.tile([P, c], U8, align_bytes=64, name="scales")
             nc.vector.quantize_mx(
-                out=codes[:].bitcast(FP8X4), scales=scales[:], in_=g[:].rearrange("p c t -> p (c t)")
+                out=codes[:].bitcast(FP8X4), scales=scales[:], in_=g[:].rearrange("p c s f -> p (c s f)")
             )
             osb = outp.tile([P, rc, OUTS], F32, name="osb")
             for q0 in range(0, rc, 4):
@@ -170,12 +177,14 @@ def tile_kan_layer_t_kernel(tc, x, spline_coeffs, out):
 
         starts = []
         r0 = 0
-        for rc, acols in CHUNKS:
+        for rc in CHUNKS:
             starts.append(r0)
             r0 += rc
-        for n, (rc, acols) in enumerate(CHUNKS):
-            tiles = front(starts[n], rc)
-            if n == 0:
-                weights()
-            g = middle(rc, acols, tiles)
+        planes = folds(0, CHUNKS[0])
+        weights()
+        for n, rc in enumerate(CHUNKS):
+            tiles = cubes(rc, planes)
+            if n + 1 < len(CHUNKS):
+                planes = folds(starts[n + 1], CHUNKS[n + 1])
+            g = values(rc, tiles)
             back(starts[n], rc, g)

@@ -30,8 +30,8 @@ def tile_kan_layer_t_kernel(tc, x, spline_coeffs, out):
     with ExitStack() as ctx:
         const = ctx.enter_context(tc.tile_pool(name="const", bufs=1))
         fold = ctx.enter_context(tc.tile_pool(name="fold", bufs=2))
-        actp = ctx.enter_context(tc.tile_pool(name="actp", bufs=2))
-        dvep = ctx.enter_context(tc.tile_pool(name="dvep", bufs=2))
+        actp = ctx.enter_context(tc.tile_pool(name="actp", bufs=3))
+        dvep = ctx.enter_context(tc.tile_pool(name="dvep", bufs=3))
         outp = ctx.enter_context(tc.tile_pool(name="outp", bufs=3))
         ps_t = ctx.enter_context(tc.psum_pool(name="ps_t", bufs=4))
         ps_u = ctx.enter_context(tc.psum_pool(name="ps_u", bufs=2))
@@ -55,6 +55,9 @@ def tile_kan_layer_t_kernel(tc, x, spline_coeffs, out):
         two_thirds = const.tile([P, 1], F32)
         nc.vector.tensor_scalar(out=two_thirds[:], in0=one[:], scalar1=2.0 / 3.0, scalar2=None, op0=ALU.mult)
 
+        shift = const.tile([P, 1], F32)
+        nc.vector.tensor_scalar(out=shift[:], in0=one[:], scalar1=-3.0 / 11, scalar2=None, op0=ALU.mult)
+
         w_codes = const.tile([P, OUTS], U32, align_bytes=64)
         w_scales = const.tile([P, OUTS], U8, align_bytes=64)
 
@@ -73,14 +76,17 @@ def tile_kan_layer_t_kernel(tc, x, spline_coeffs, out):
                 out=w_codes[:].bitcast(FP8X4), scales=w_scales[:], in_=wq[:].rearrange("p o t -> p (o t)")
             )
 
-        def folds(r0, rc):
+        def folds(r0, rc, on_scalar):
             sg = fold.tile([P, rc, FEAT // 4, 2, 4], F32, name="sg")
             xin = x_sb[:, r0 : r0 + rc, :].rearrange("p r (a j) -> p r a j", j=4)
             for h in range(2):
                 nc.scalar.activation(out=sg[:, :, :, h, :], in_=xin, func=AF.Sigmoid, scale=2.0 - 4.0 * h)
             s = sg[:].rearrange("p r a h j -> p (r a h j)")
             m = fold.tile([P, rc * P], F32, name="m")
-            nc.vector.tensor_scalar(out=m[:], in0=s, scalar1=-0.5, scalar2=-3.0 / 11, op0=ALU.mult, op1=ALU.add)
+            if on_scalar:
+                nc.scalar.activation(out=m[:], in_=s, func=AF.Identity, bias=shift[:, 0:1], scale=-0.5)
+            else:
+                nc.vector.tensor_scalar(out=m[:], in0=s, scalar1=-0.5, scalar2=-3.0 / 11, op0=ALU.mult, op1=ALU.add)
             ca = fold.tile([P, rc * P], F32, name="ca")
             nc.vector.tensor_scalar(out=ca[:], in0=s, scalar1=2.0 / 11, scalar2=6.0 / 11, op0=ALU.max, op1=ALU.min)
             cb = fold.tile([P, rc * P], F32, name="cb")
@@ -180,11 +186,17 @@ def tile_kan_layer_t_kernel(tc, x, spline_coeffs, out):
         for rc in CHUNKS:
             starts.append(r0)
             r0 += rc
-        planes = folds(0, CHUNKS[0])
+        planes = folds(0, CHUNKS[0], False)
         weights()
+        done = None
         for n, rc in enumerate(CHUNKS):
-            tiles = cubes(rc, planes)
+            mine = planes
             if n + 1 < len(CHUNKS):
-                planes = folds(starts[n + 1], CHUNKS[n + 1])
-            g = values(rc, tiles)
-            back(starts[n], rc, g)
+                planes = folds(starts[n + 1], CHUNKS[n + 1], n % 2 == 0)
+            tiles = cubes(rc, mine)
+            if n:
+                g = values(CHUNKS[n - 1], done)
+                back(starts[n - 1], CHUNKS[n - 1], g)
+            done = tiles
+        g = values(CHUNKS[-1], done)
+        back(starts[-1], CHUNKS[-1], g)

@@ -17,8 +17,8 @@ P = 128
 ROWS = 128
 FEAT = 64
 OUTS = 128
-CHUNKS = (2, 2, 4) + (8,) * 14 + (4, 2, 2)
-LOADS = ((0, 2), (2, 8), (8, 32), (32, 64), (64, 128))
+CHUNKS = (4,) + (8,) * 15 + (4,)
+LOADS = ((0, 4), (4, 12), (12, 32), (32, 64), (64, 128))
 SLOT_K = (4, 6, 0, 2)
 assert sum(CHUNKS) == ROWS
 
@@ -50,10 +50,25 @@ def tile_kan_layer_t_kernel(tc, x, spline_coeffs, out):
         nc.vector.tensor_copy(out=ident_b[:], in_=ident[:])
         one = const.tile([P, 1], F32)
         nc.vector.memset(one[:], 1.0)
-        neg = const.tile([P, 1], F32)
-        nc.vector.memset(neg[:], -1.0)
-        two_thirds = const.tile([P, 1], F32)
-        nc.vector.tensor_scalar(out=two_thirds[:], in0=one[:], scalar1=2.0 / 3.0, scalar2=None, op0=ALU.mult)
+        half_neg = const.tile([P, 1], F32)
+        nc.vector.memset(half_neg[:], -0.5)
+        three_halves = const.tile([P, 1], F32)
+        nc.vector.memset(three_halves[:], 1.5)
+        root2 = const.tile([P, 1], F32)
+        nc.vector.tensor_scalar(out=root2[:], in0=one[:], scalar1=2.0**0.5, scalar2=None, op0=ALU.mult)
+        par = const.tile([P, 1], F32)
+        nc.vector.tensor_reduce(
+            out=par[:],
+            in_=ident[:].rearrange("p (a h j) -> p a h j", h=2, j=4)[:, :, 1, :],
+            axis=mybir.AxisListType.XY,
+            op=ALU.add,
+        )
+        g_scale = const.tile([P, 1], F32)
+        nc.vector.tensor_scalar(out=g_scale[:], in0=par[:], scalar1=1.0, scalar2=-0.5, op0=ALU.mult, op1=ALU.add)
+        g_bias = const.tile([P, 1], F32)
+        nc.vector.tensor_scalar(
+            out=g_bias[:], in0=par[:], scalar1=1.0 / 24 - 2.0 / 3, scalar2=2.0 / 3, op0=ALU.mult, op1=ALU.add
+        )
 
         shift = const.tile([P, 1], F32)
         nc.vector.tensor_scalar(out=shift[:], in0=one[:], scalar1=-3.0 / 11, scalar2=None, op0=ALU.mult)
@@ -83,10 +98,7 @@ def tile_kan_layer_t_kernel(tc, x, spline_coeffs, out):
                 nc.scalar.activation(out=sg[:, :, :, h, :], in_=xin, func=AF.Sigmoid, scale=2.0 - 4.0 * h)
             s = sg[:].rearrange("p r a h j -> p (r a h j)")
             m = fold.tile([P, rc * P], F32, name="m")
-            if on_scalar:
-                nc.scalar.activation(out=m[:], in_=s, func=AF.Identity, bias=shift[:, 0:1], scale=-0.5)
-            else:
-                nc.vector.tensor_scalar(out=m[:], in0=s, scalar1=-0.5, scalar2=-3.0 / 11, op0=ALU.mult, op1=ALU.add)
+            nc.scalar.activation(out=m[:], in_=s, func=AF.Identity, bias=shift[:, 0:1], scale=-0.5)
             ca = fold.tile([P, rc * P], F32, name="ca")
             nc.vector.tensor_scalar(out=ca[:], in0=s, scalar1=2.0 / 11, scalar2=6.0 / 11, op0=ALU.max, op1=ALU.min)
             cb = fold.tile([P, rc * P], F32, name="cb")
@@ -95,7 +107,30 @@ def tile_kan_layer_t_kernel(tc, x, spline_coeffs, out):
             nc.vector.tensor_scalar(out=na[:], in0=m[:], scalar1=1.0 / 11, scalar2=-6.0 / 11, op0=ALU.add, op1=ALU.max)
             nb = fold.tile([P, rc * P], F32, name="nb")
             nc.vector.tensor_scalar(out=nb[:], in0=m[:], scalar1=-8.0 / 11, scalar2=-4.0 / 11, op0=ALU.max, op1=ALU.min)
-            return m, ca, cb, na, nb
+            half = [P, rc * FEAT // 4, 4]
+            tb = fold.tile(half, F32, name="tb")
+            even = [t[:].rearrange("p (n h j) -> p n h j", h=2, j=4)[:, :, 0, :] for t in (cb, m)]
+            nc.vector.tensor_tensor(out=tb[:], in0=even[0], in1=even[1], op=ALU.add)
+            ee = fold.tile(half, F32, name="ee")
+            nc.scalar.activation(out=ee[:], in_=tb[:], func=AF.Abs, scale=22.0)
+            yh = fold.tile(half, F32, name="yh")
+            nc.scalar.activation(out=yh[:], in_=ee[:], func=AF.Abs, bias=half_neg[:, 0:1], scale=0.5)
+            q1 = fold.tile([P, rc * FEAT // 4, 2, 4], F32, name="q1")
+            nc.scalar.activation(
+                out=q1[:, :, 0, :], in_=yh[:], func=AF.Square, bias=root2[:, 0:1], scale=-2.0 * 2.0**0.5
+            )
+            nc.scalar.activation(
+                out=q1[:, :, 1, :], in_=yh[:], func=AF.Square, bias=three_halves[:, 0:1], scale=-2.0
+            )
+            q2 = fold.tile([P, rc * FEAT // 4, 2, 4], F32, name="q2")
+            nc.vector.scalar_tensor_tensor(
+                out=q2[:, :, 0, :], in0=yh[:], scalar=0.5, in1=q1[:, :, 0, :], op0=ALU.subtract, op1=ALU.mult
+            )
+            if on_scalar:
+                nc.scalar.copy(out=q2[:, :, 1, :], in_=q2[:, :, 0, :])
+            else:
+                nc.vector.tensor_copy(out=q2[:, :, 1, :], in_=q2[:, :, 0, :])
+            return ca, cb, na, nb, q1[:].rearrange("p n h j -> p (n h j)"), q2[:].rearrange("p n h j -> p (n h j)")
 
         def add_t(dst, one_plane, other_plane, r):
             for n, plane in enumerate((one_plane, other_plane)):
@@ -104,19 +139,13 @@ def tile_kan_layer_t_kernel(tc, x, spline_coeffs, out):
                 )
 
         def cubes(rc, planes):
-            m, ca, cb, na, nb = planes
+            ca, cb, na, nb, q1, q2 = planes
             c = rc * P
             t2 = actp.tile([P, c, 2], F32, name="t2")
             t3 = dvep.tile([P, c, 2], BF16, name="t3")
-            ee = actp.tile([P, c], F32, name="ee")
+            gd = actp.tile([P, c, 2], BF16, name="gd")
             for q0 in range(0, rc, 4):
                 n = min(4, rc - q0)
-                uu = ps_u.tile([P, n, P], F32, name="uu")
-                for r in range(n):
-                    add_t(uu[:, r, :], cb, m, q0 + r)
-                nc.scalar.activation(
-                    out=ee[:, q0 * P : (q0 + n) * P], in_=uu[:].rearrange("p r c -> p (r c)"), func=AF.Abs, scale=22.0
-                )
                 for p0 in range(q0, q0 + n, 2):
                     tt = ps_t.tile([P, 2, 2, P], F32, name="tt")
                     for r in range(2):
@@ -128,20 +157,23 @@ def tile_kan_layer_t_kernel(tc, x, spline_coeffs, out):
                         out=t2[:, cols, :], in_=tv, func=AF.Square, scale=(22.0**3 / 6.0) ** 0.5
                     )
                     nc.vector.tensor_tensor(out=t3[:, cols, :], in0=tv, in1=t2[:, cols, :], op=ALU.mult)
-            yy = actp.tile([P, c], F32, name="yy")
-            nc.scalar.activation(out=yy[:], in_=ee[:], func=AF.Abs, bias=neg[:, 0:1])
-            vv = actp.tile([P, c], F32, name="vv")
-            nc.scalar.activation(out=vv[:], in_=yy[:], func=AF.Square, bias=one[:, 0:1], scale=-1.0)
-            return t3, yy, vv
+            for q0 in range(0, rc, 4):
+                n = min(4, rc - q0)
+                uu = ps_u.tile([P, n, P], F32, name="uu")
+                for r in range(n):
+                    add_t(uu[:, r, :], q1, q2, q0 + r)
+                nc.scalar.activation(
+                    out=gd[:, q0 * P : (q0 + n) * P, :],
+                    in_=uu[:].rearrange("p r c -> p (r c)").unsqueeze(2).to_broadcast([P, n * P, 2]),
+                    func=AF.Identity,
+                    bias=g_bias[:, 0:1],
+                    scale=g_scale[:, 0:1],
+                )
+            return t3, gd
 
         def values(rc, tiles):
-            t3, yy, vv = tiles
+            t3, gd = tiles
             c = rc * P
-            nc.vector.scalar_tensor_tensor(out=vv[:], in0=yy[:], scalar=1.0, in1=vv[:], op0=ALU.add, op1=ALU.mult)
-            gd = actp.tile([P, c, 2], BF16, name="gd")
-            nc.scalar.activation(
-                out=gd[:], in_=vv[:].unsqueeze(2).to_broadcast([P, c, 2]), func=AF.Identity, bias=two_thirds[:, 0:1], scale=-0.5
-            )
             pp = dvep.tile([P, 2, c, 2], BF16, name="pp")
             for s in range(2):
                 nc.vector.tensor_scalar(

@@ -59,8 +59,8 @@ def tile_kan_layer_t_kernel(tc, x, spline_coeffs, out):
         par = const.tile([P, 1], F32)
         nc.vector.tensor_reduce(
             out=par[:],
-            in_=ident[:].rearrange("p (a h j) -> p a h j", h=2, j=4)[:, :, 1, :],
-            axis=mybir.AxisListType.XY,
+            in_=ident[:, FEAT:P],
+            axis=mybir.AxisListType.X,
             op=ALU.add,
         )
         g_scale = const.tile([P, 1], F32)
@@ -77,26 +77,34 @@ def tile_kan_layer_t_kernel(tc, x, spline_coeffs, out):
         w_scales = const.tile([P, OUTS], U8, align_bytes=64)
 
         def weights():
-            w4 = w_sb[:].rearrange("o (a j k) -> o a j k", j=4, k=8)
-            wg = const.tile([P, 4, FEAT // 4, 2, 4], BF16)
+            w4 = w_sb[:].rearrange("o (u l j k) -> o l u j k", l=4, j=4, k=8)
+            wg = const.tile([P, 4, 2, FEAT], BF16)
             for t in range(4):
-                nc.vector.tensor_copy(out=wg[:, t, :, 0, :], in_=w4[:, :, :, SLOT_K[t]])
-                nc.vector.tensor_copy(out=wg[:, t, :, 1, :], in_=w4[:, :, :, 7 - SLOT_K[t]])
+                for h, k in enumerate((SLOT_K[t], 7 - SLOT_K[t])):
+                    nc.vector.tensor_copy(
+                        out=wg[:, t, h, :].rearrange("o (l u j) -> o l u j", l=4, j=4), in_=w4[:, :, :, :, k]
+                    )
             w_t = ps_o.tile([P, 4, OUTS], BF16, name="acc")
             for t in range(4):
-                nc.tensor.transpose(w_t[:, t, :], wg[:, t, :, :, :].rearrange("o a h j -> o (a h j)"), ident_b[:])
+                nc.tensor.transpose(w_t[:, t, :], wg[:, t, :, :].rearrange("o h f -> o (h f)"), ident_b[:])
             wq = const.tile([P, OUTS, 4], BF16, align_bytes=64)
             nc.vector.tensor_copy(out=wq[:], in_=w_t[:].rearrange("p t o -> p o t"))
             nc.vector.quantize_mx(
                 out=w_codes[:].bitcast(FP8X4), scales=w_scales[:], in_=wq[:].rearrange("p o t -> p (o t)")
             )
 
-        def folds(r0, rc, on_scalar):
-            sg = fold.tile([P, rc, FEAT // 4, 2, 4], F32, name="sg")
-            xin = x_sb[:, r0 : r0 + rc, :].rearrange("p r (a j) -> p r a j", j=4)
+        def folds(r0, rc):
+            sg = fold.tile([P, rc, 2, FEAT], F32, name="sg")
+            xin = x_sb[:, r0 : r0 + rc, :].rearrange("p r (u l j) -> p r l u j", l=4, j=4)
             for h in range(2):
-                nc.scalar.activation(out=sg[:, :, :, h, :], in_=xin, func=AF.Sigmoid, scale=2.0 - 4.0 * h)
-            s = sg[:].rearrange("p r a h j -> p (r a h j)")
+                for cl in range(4):
+                    nc.scalar.activation(
+                        out=sg[:, :, h, 16 * cl : 16 * cl + 16].rearrange("p r (u j) -> p r u j", j=4),
+                        in_=xin[:, :, cl, :, :],
+                        func=AF.Sigmoid,
+                        scale=2.0 - 4.0 * h,
+                    )
+            s = sg[:].rearrange("p r h f -> p (r h f)")
             m = fold.tile([P, rc * P], F32, name="m")
             nc.scalar.activation(out=m[:], in_=s, func=AF.Identity, bias=shift[:, 0:1], scale=-0.5)
             ca = fold.tile([P, rc * P], F32, name="ca")
@@ -107,30 +115,27 @@ def tile_kan_layer_t_kernel(tc, x, spline_coeffs, out):
             nc.vector.tensor_scalar(out=na[:], in0=m[:], scalar1=1.0 / 11, scalar2=-6.0 / 11, op0=ALU.add, op1=ALU.max)
             nb = fold.tile([P, rc * P], F32, name="nb")
             nc.vector.tensor_scalar(out=nb[:], in0=m[:], scalar1=-8.0 / 11, scalar2=-4.0 / 11, op0=ALU.max, op1=ALU.min)
-            half = [P, rc * FEAT // 4, 4]
+            half = [P, rc, FEAT]
             tb = fold.tile(half, F32, name="tb")
-            even = [t[:].rearrange("p (n h j) -> p n h j", h=2, j=4)[:, :, 0, :] for t in (cb, m)]
+            even = [t[:].rearrange("p (r h f) -> p r h f", h=2, f=FEAT)[:, :, 0, :] for t in (cb, m)]
             nc.vector.tensor_tensor(out=tb[:], in0=even[0], in1=even[1], op=ALU.add)
             ee = fold.tile(half, F32, name="ee")
             nc.scalar.activation(out=ee[:], in_=tb[:], func=AF.Abs, scale=22.0)
             yh = fold.tile(half, F32, name="yh")
             nc.scalar.activation(out=yh[:], in_=ee[:], func=AF.Abs, bias=half_neg[:, 0:1], scale=0.5)
-            q1 = fold.tile([P, rc * FEAT // 4, 2, 4], F32, name="q1")
+            q1 = fold.tile([P, rc, 2, FEAT], F32, name="q1")
             nc.scalar.activation(
                 out=q1[:, :, 0, :], in_=yh[:], func=AF.Square, bias=root2[:, 0:1], scale=-2.0 * 2.0**0.5
             )
             nc.scalar.activation(
                 out=q1[:, :, 1, :], in_=yh[:], func=AF.Square, bias=three_halves[:, 0:1], scale=-2.0
             )
-            q2 = fold.tile([P, rc * FEAT // 4, 2, 4], F32, name="q2")
+            q2 = fold.tile([P, rc, 2, FEAT], F32, name="q2")
             nc.vector.scalar_tensor_tensor(
                 out=q2[:, :, 0, :], in0=yh[:], scalar=0.5, in1=q1[:, :, 0, :], op0=ALU.subtract, op1=ALU.mult
             )
-            if on_scalar:
-                nc.scalar.copy(out=q2[:, :, 1, :], in_=q2[:, :, 0, :])
-            else:
-                nc.vector.tensor_copy(out=q2[:, :, 1, :], in_=q2[:, :, 0, :])
-            return ca, cb, na, nb, q1[:].rearrange("p n h j -> p (n h j)"), q2[:].rearrange("p n h j -> p (n h j)")
+            nc.sync.dma_start(out=q2[:, :, 1, :], in_=q2[:, :, 0, :])
+            return ca, cb, na, nb, q1[:].rearrange("p r h f -> p (r h f)"), q2[:].rearrange("p r h f -> p (r h f)")
 
         def add_t(dst, one_plane, other_plane, r):
             for n, plane in enumerate((one_plane, other_plane)):
@@ -218,13 +223,13 @@ def tile_kan_layer_t_kernel(tc, x, spline_coeffs, out):
         for rc in CHUNKS:
             starts.append(r0)
             r0 += rc
-        planes = folds(0, CHUNKS[0], False)
+        planes = folds(0, CHUNKS[0])
         weights()
         done = None
         for n, rc in enumerate(CHUNKS):
             mine = planes
             if n + 1 < len(CHUNKS):
-                planes = folds(starts[n + 1], CHUNKS[n + 1], n % 2 == 0)
+                planes = folds(starts[n + 1], CHUNKS[n + 1])
             tiles = cubes(rc, mine)
             if n:
                 g = values(CHUNKS[n - 1], done)

@@ -94,30 +94,25 @@ def tile_kan_layer_t_kernel(tc, x, spline_coeffs, out):
             )
 
         def folds(r0, rc):
-            sg = fold.tile([P, rc, 2, FEAT], F32, name="sg")
-            xin = x_sb[:, r0 : r0 + rc, :].rearrange("p r (u l j) -> p r l u j", l=4, j=4)
+            sg = fold.tile([P, 2, 4, rc * 4, 4], F32, name="sg")
+            xin = x_sb[:, r0 : r0 + rc, :].rearrange("p r (u l j) -> p l (r u) j", l=4, j=4)
             for h in range(2):
-                for cl in range(4):
-                    nc.scalar.activation(
-                        out=sg[:, :, h, 16 * cl : 16 * cl + 16].rearrange("p r (u j) -> p r u j", j=4),
-                        in_=xin[:, :, cl, :, :],
-                        func=AF.Sigmoid,
-                        scale=2.0 - 4.0 * h,
-                    )
-            s = sg[:].rearrange("p r h f -> p (r h f)")
-            m = fold.tile([P, rc * P], F32, name="m")
-            nc.scalar.activation(out=m[:], in_=s, func=AF.Identity, bias=shift[:, 0:1], scale=-0.5)
-            ca = fold.tile([P, rc * P], F32, name="ca")
-            nc.vector.tensor_scalar(out=ca[:], in0=s, scalar1=2.0 / 11, scalar2=6.0 / 11, op0=ALU.max, op1=ALU.min)
-            cb = fold.tile([P, rc * P], F32, name="cb")
-            nc.vector.tensor_scalar(out=cb[:], in0=s, scalar1=4.0 / 11, scalar2=8.0 / 11, op0=ALU.max, op1=ALU.min)
+                nc.scalar.activation(out=sg[:, h, :, :, :], in_=xin, func=AF.Sigmoid, scale=2.0 - 4.0 * h)
+            s = sg[:].rearrange("p h l (r u) j -> p r (h l) (u j)", u=4)
+            m_t = fold.tile([P, rc, 8, 16], F32, name="m_t")
+            nc.scalar.activation(out=m_t[:], in_=s, func=AF.Identity, bias=shift[:, 0:1], scale=-0.5)
+            ca_t = fold.tile([P, rc, 8, 16], F32, name="ca_t")
+            nc.vector.tensor_scalar(out=ca_t[:], in0=s, scalar1=2.0 / 11, scalar2=6.0 / 11, op0=ALU.max, op1=ALU.min)
+            cb_t = fold.tile([P, rc, 8, 16], F32, name="cb_t")
+            nc.vector.tensor_scalar(out=cb_t[:], in0=s, scalar1=4.0 / 11, scalar2=8.0 / 11, op0=ALU.max, op1=ALU.min)
+            m, ca, cb = (t[:].rearrange("p r k f -> p (r k f)") for t in (m_t, ca_t, cb_t))
             na = fold.tile([P, rc * P], F32, name="na")
-            nc.vector.tensor_scalar(out=na[:], in0=m[:], scalar1=1.0 / 11, scalar2=-6.0 / 11, op0=ALU.add, op1=ALU.max)
+            nc.vector.tensor_scalar(out=na[:], in0=m, scalar1=1.0 / 11, scalar2=-6.0 / 11, op0=ALU.add, op1=ALU.max)
             nb = fold.tile([P, rc * P], F32, name="nb")
-            nc.vector.tensor_scalar(out=nb[:], in0=m[:], scalar1=-8.0 / 11, scalar2=-4.0 / 11, op0=ALU.max, op1=ALU.min)
+            nc.vector.tensor_scalar(out=nb[:], in0=m, scalar1=-8.0 / 11, scalar2=-4.0 / 11, op0=ALU.max, op1=ALU.min)
             half = [P, rc, FEAT]
             tb = fold.tile(half, F32, name="tb")
-            even = [t[:].rearrange("p (r h f) -> p r h f", h=2, f=FEAT)[:, :, 0, :] for t in (cb, m)]
+            even = [t.rearrange("p (r h f) -> p r h f", h=2, f=FEAT)[:, :, 0, :] for t in (cb, m)]
             nc.vector.tensor_tensor(out=tb[:], in0=even[0], in1=even[1], op=ALU.add)
             ee = fold.tile(half, F32, name="ee")
             nc.scalar.activation(out=ee[:], in_=tb[:], func=AF.Abs, scale=22.0)

@@ -17,8 +17,8 @@ P = 128
 ROWS = 128
 FEAT = 64
 OUTS = 128
-CHUNKS = (4,) + (8,) * 15 + (4,)
-LOADS = ((0, 4), (4, 12), (12, 32), (32, 64), (64, 128))
+CHUNKS = (8,) * 16
+LOADS = ((0, 8), (8, 16), (16, 32), (32, 64), (64, 128))
 SLOT_K = (4, 6, 0, 2)
 assert sum(CHUNKS) == ROWS
 
@@ -188,30 +188,34 @@ def tile_kan_layer_t_kernel(tc, x, spline_coeffs, out):
             )
             return g
 
-        def back(r0, rc, g):
-            c = rc * P
-            codes = dvep.tile([P, c], U32, align_bytes=64, name="codes")
-            scales = dvep.tile([P, c], U8, align_bytes=64, name="scales")
-            nc.vector.quantize_mx(
-                out=codes[:].bitcast(FP8X4), scales=scales[:], in_=g[:].rearrange("p c s f -> p (c s f)")
-            )
+        def back(r0, rc, g, piece):
+            codes = dvep.tile([P, rc * P], U32, align_bytes=64, name="codes")
+            scales = dvep.tile([P, rc * P], U8, align_bytes=64, name="scales")
             osb = outp.tile([P, rc, OUTS], F32, name="osb")
-            for q0 in range(0, rc, 4):
-                n = min(4, rc - q0)
-                acc = ps_o.tile([P, n, OUTS], F32, name="acc")
-                for j in range(n):
-                    c0 = (q0 + j) * P
-                    nc.tensor.matmul_mx(
-                        out=acc[:, j, :],
-                        lhsT=codes[:, c0 : c0 + P].bitcast(FP8X4),
-                        lhsT_scale=scales[:, c0 : c0 + P],
-                        rhs=w_codes[:].bitcast(FP8X4),
-                        rhs_scale=w_scales[:],
-                        start=True,
-                        stop=True,
-                    )
-                nc.scalar.copy(out=osb[:, q0 : q0 + n, :], in_=acc[:])
-            nc.sync.dma_start(out=out_v[:, r0 : r0 + rc, :], in_=osb[:])
+            gf = g[:].rearrange("p c s f -> p (c s f)")
+            for a in range(0, rc, piece):
+                b = a + piece
+                nc.vector.quantize_mx(
+                    out=codes[:, a * P : b * P].bitcast(FP8X4),
+                    scales=scales[:, a * P : b * P],
+                    in_=gf[:, 4 * a * P : 4 * b * P],
+                )
+                for q0 in range(a, b, 4):
+                    n = min(4, b - q0)
+                    acc = ps_o.tile([P, n, OUTS], F32, name="acc")
+                    for j in range(n):
+                        c0 = (q0 + j) * P
+                        nc.tensor.matmul_mx(
+                            out=acc[:, j, :],
+                            lhsT=codes[:, c0 : c0 + P].bitcast(FP8X4),
+                            lhsT_scale=scales[:, c0 : c0 + P],
+                            rhs=w_codes[:].bitcast(FP8X4),
+                            rhs_scale=w_scales[:],
+                            start=True,
+                            stop=True,
+                        )
+                    nc.scalar.copy(out=osb[:, q0 : q0 + n, :], in_=acc[:])
+                nc.sync.dma_start(out=out_v[:, r0 + a : r0 + b, :], in_=osb[:, a:b, :])
 
         starts = []
         r0 = 0
@@ -228,7 +232,7 @@ def tile_kan_layer_t_kernel(tc, x, spline_coeffs, out):
             tiles = cubes(rc, mine)
             if n:
                 g = values(CHUNKS[n - 1], done)
-                back(starts[n - 1], CHUNKS[n - 1], g)
+                back(starts[n - 1], CHUNKS[n - 1], g, CHUNKS[n - 1])
             done = tiles
         g = values(CHUNKS[-1], done)
-        back(starts[-1], CHUNKS[-1], g)
+        back(starts[-1], CHUNKS[-1], g, 2)

@@ -30,6 +30,8 @@ def tile_kan_layer_t_kernel(tc, x, spline_coeffs, out):
     with ExitStack() as ctx:
         const = ctx.enter_context(tc.tile_pool(name="const", bufs=1))
         fold = ctx.enter_context(tc.tile_pool(name="fold", bufs=2))
+        sgp = ctx.enter_context(tc.tile_pool(name="sgp", bufs=3))
+        half_slope = ctx.enter_context(tc.tile_pool(name="half_slope", bufs=1))
         actp = ctx.enter_context(tc.tile_pool(name="actp", bufs=3))
         dvep = ctx.enter_context(tc.tile_pool(name="dvep", bufs=3))
         outp = ctx.enter_context(tc.tile_pool(name="outp", bufs=3))
@@ -52,6 +54,11 @@ def tile_kan_layer_t_kernel(tc, x, spline_coeffs, out):
         nc.vector.memset(one[:], 1.0)
         half_neg = const.tile([P, 1], F32)
         nc.vector.memset(half_neg[:], -0.5)
+        fold_bias = []
+        for n, value in enumerate((-6.0, -4.0, -2.0)):
+            bias_t = const.tile([P, 1], F32, name="fold_bias%d" % n)
+            nc.vector.memset(bias_t[:], value)
+            fold_bias.append(bias_t)
         three_halves = const.tile([P, 1], F32)
         nc.vector.memset(three_halves[:], 1.5)
         root2 = const.tile([P, 1], F32)
@@ -69,9 +76,6 @@ def tile_kan_layer_t_kernel(tc, x, spline_coeffs, out):
         nc.vector.tensor_scalar(
             out=g_bias[:], in0=par[:], scalar1=1.0 / 24 - 2.0 / 3, scalar2=2.0 / 3, op0=ALU.mult, op1=ALU.add
         )
-
-        shift = const.tile([P, 1], F32)
-        nc.vector.tensor_scalar(out=shift[:], in0=one[:], scalar1=-3.0 / 11, scalar2=None, op0=ALU.mult)
 
         w_codes = const.tile([P, OUTS], U32, align_bytes=64)
         w_scales = const.tile([P, OUTS], U8, align_bytes=64)
@@ -93,44 +97,78 @@ def tile_kan_layer_t_kernel(tc, x, spline_coeffs, out):
                 out=w_codes[:].bitcast(FP8X4), scales=w_scales[:], in_=wq[:].rearrange("p o t -> p (o t)")
             )
 
-        def folds(r0, rc):
-            sg = fold.tile([P, 2, 4, rc * 4, 4], F32, name="sg")
+        def sigmoids(r0, rc):
+            sg = sgp.tile([P, 2, 4, rc * 4, 4], F32, name="sg")
             xin = x_sb[:, r0 : r0 + rc, :].rearrange("p r (u l j) -> p l (r u) j", l=4, j=4)
             for h in range(2):
                 nc.scalar.activation(out=sg[:, h, :, :, :], in_=xin, func=AF.Sigmoid, scale=2.0 - 4.0 * h)
-            s = sg[:].rearrange("p h l (r u) j -> p r (h l) (u j)", u=4)
-            m_t = fold.tile([P, rc, 8, 16], F32, name="m_t")
-            nc.scalar.activation(out=m_t[:], in_=s, func=AF.Identity, bias=shift[:, 0:1], scale=-0.5)
-            ca_t = fold.tile([P, rc, 8, 16], F32, name="ca_t")
-            nc.vector.tensor_scalar(out=ca_t[:], in0=s, scalar1=2.0 / 11, scalar2=6.0 / 11, op0=ALU.max, op1=ALU.min)
-            cb_t = fold.tile([P, rc, 8, 16], F32, name="cb_t")
-            nc.vector.tensor_scalar(out=cb_t[:], in0=s, scalar1=4.0 / 11, scalar2=8.0 / 11, op0=ALU.max, op1=ALU.min)
-            m, ca, cb = (t[:].rearrange("p r k f -> p (r k f)") for t in (m_t, ca_t, cb_t))
-            na = fold.tile([P, rc * P], F32, name="na")
-            nc.vector.tensor_scalar(out=na[:], in0=m, scalar1=1.0 / 11, scalar2=-6.0 / 11, op0=ALU.add, op1=ALU.max)
-            nb = fold.tile([P, rc * P], F32, name="nb")
-            nc.vector.tensor_scalar(out=nb[:], in0=m, scalar1=-8.0 / 11, scalar2=-4.0 / 11, op0=ALU.max, op1=ALU.min)
-            half = [P, rc, FEAT]
-            tb = fold.tile(half, F32, name="tb")
-            even = [t.rearrange("p (r h f) -> p r h f", h=2, f=FEAT)[:, :, 0, :] for t in (cb, m)]
-            nc.vector.tensor_tensor(out=tb[:], in0=even[0], in1=even[1], op=ALU.add)
-            ee = fold.tile(half, F32, name="ee")
-            nc.scalar.activation(out=ee[:], in_=tb[:], func=AF.Abs, scale=22.0)
-            yh = fold.tile(half, F32, name="yh")
-            nc.scalar.activation(out=yh[:], in_=ee[:], func=AF.Abs, bias=half_neg[:, 0:1], scale=0.5)
+            return sg[:].rearrange("p h l (r u) j -> p r (h l) (u j)", u=4)
+
+        def half_slopes(rc, s):
+            m_t = half_slope.tile([P, rc, 8, 16], F32, name="m_t")
+            nc.gpsimd.tensor_scalar(
+                out=m_t[:], in0=s, scalar1=-0.5, scalar2=-3.0 / 11, op0=ALU.mult, op1=ALU.add
+            )
+            return m_t
+
+        def clamp(rc, name, src, op0, scalar1, op1, scalar2):
+            t = fold.tile([P, rc, 8, 16], F32, name=name)
+            nc.vector.tensor_scalar(out=t[:], in0=src, scalar1=scalar1, scalar2=scalar2, op0=op0, op1=op1)
+            return t
+
+        def flat(t):
+            return t[:].rearrange("p r k f -> p (r k f)")
+
+        def fold_steps(rc, s):
+            ee = fold.tile([P, rc, FEAT], F32, name="ee")
+            biases = fold_bias + [half_neg]
+            steps = [
+                lambda: nc.scalar.activation(
+                    out=ee[:].rearrange("p r (l f) -> p r l f", l=4),
+                    in_=s[:, :, 0:4, :],
+                    func=AF.Abs,
+                    bias=biases[0][:, 0:1],
+                    scale=11.0,
+                )
+            ]
+            for n in range(1, 4):
+                steps.append(
+                    lambda n=n: nc.scalar.activation(
+                        out=ee[:], in_=ee[:], func=AF.Abs, bias=biases[n][:, 0:1], scale=(1.0, 0.5)[n // 3]
+                    )
+                )
+            return ee, steps
+
+        def fold_sum(rc, cb, m):
+            ee = fold.tile([P, rc, FEAT], F32, name="ee")
+            even = [flat(t).rearrange("p (r h f) -> p r h f", h=2, f=FEAT)[:, :, 0, :] for t in (cb, m)]
+            nc.vector.tensor_tensor(out=ee[:], in0=even[0], in1=even[1], op=ALU.add)
+            return ee
+
+        def fold_rest(ee):
+            return [
+                lambda: nc.scalar.activation(out=ee[:], in_=ee[:], func=AF.Abs, scale=22.0),
+                lambda: nc.scalar.activation(out=ee[:], in_=ee[:], func=AF.Abs, bias=half_neg[:, 0:1], scale=0.5),
+            ]
+
+        def square_steps(rc, yh):
             q1 = fold.tile([P, rc, 2, FEAT], F32, name="q1")
-            nc.scalar.activation(
-                out=q1[:, :, 0, :], in_=yh[:], func=AF.Square, bias=root2[:, 0:1], scale=-2.0 * 2.0**0.5
-            )
-            nc.scalar.activation(
-                out=q1[:, :, 1, :], in_=yh[:], func=AF.Square, bias=three_halves[:, 0:1], scale=-2.0
-            )
+            return q1, [
+                lambda: nc.scalar.activation(
+                    out=q1[:, :, 0, :], in_=yh[:], func=AF.Square, bias=root2[:, 0:1], scale=-2.0 * 2.0**0.5
+                ),
+                lambda: nc.scalar.activation(
+                    out=q1[:, :, 1, :], in_=yh[:], func=AF.Square, bias=three_halves[:, 0:1], scale=-2.0
+                ),
+            ]
+
+        def centre_cube(rc, yh, q1):
             q2 = fold.tile([P, rc, 2, FEAT], F32, name="q2")
             nc.vector.scalar_tensor_tensor(
                 out=q2[:, :, 0, :], in0=yh[:], scalar=0.5, in1=q1[:, :, 0, :], op0=ALU.subtract, op1=ALU.mult
             )
             nc.sync.dma_start(out=q2[:, :, 1, :], in_=q2[:, :, 0, :])
-            return ca, cb, na, nb, q1[:].rearrange("p r h f -> p (r h f)"), q2[:].rearrange("p r h f -> p (r h f)")
+            return q2
 
         def add_t(dst, one_plane, other_plane, r):
             for n, plane in enumerate((one_plane, other_plane)):
@@ -138,47 +176,62 @@ def tile_kan_layer_t_kernel(tc, x, spline_coeffs, out):
                     dst, lhsT=plane[:, r * P : (r + 1) * P], rhs=ident[:], start=n == 0, stop=n == 1, is_transpose=True
                 )
 
-        def cubes(rc, planes):
-            ca, cb, na, nb, q1, q2 = planes
-            c = rc * P
-            t2 = actp.tile([P, c, 2], F32, name="t2")
-            t3 = dvep.tile([P, c, 2], BF16, name="t3")
-            gd = actp.tile([P, c, 2], BF16, name="gd")
+        def distances(rc, ca, cb, na, nb):
+            banks = []
+            for p0 in range(0, rc, 2):
+                tt = ps_t.tile([P, 2, 2, P], F32, name="tt")
+                for r in range(2):
+                    add_t(tt[:, 0, r, :], ca, na, p0 + r)
+                    add_t(tt[:, 1, r, :], cb, nb, p0 + r)
+                banks.append(tt[:].rearrange("p s r c -> p (r c) s"))
+            return banks
+
+        def bank_squares(rc, banks):
+            t2 = actp.tile([P, rc * P, 2], F32, name="t2")
+            for b, tv in enumerate(banks):
+                cols = slice(2 * b * P, (2 * b + 2) * P)
+                nc.scalar.activation(out=t2[:, cols, :], in_=tv, func=AF.Square, scale=(22.0**3 / 6.0) ** 0.5)
+            return t2
+
+        def cubes(rc, banks, t2):
+            t3 = dvep.tile([P, rc * P, 2], BF16, name="t3")
+            for b, tv in enumerate(banks):
+                cols = slice(2 * b * P, (2 * b + 2) * P)
+                nc.vector.tensor_tensor(out=t3[:, cols, :], in0=tv, in1=t2[:, cols, :], op=ALU.mult)
+            return t3
+
+        def centre_sums(rc, q1, q2):
+            banks = []
             for q0 in range(0, rc, 4):
-                n = min(4, rc - q0)
-                for p0 in range(q0, q0 + n, 2):
-                    tt = ps_t.tile([P, 2, 2, P], F32, name="tt")
-                    for r in range(2):
-                        add_t(tt[:, 0, r, :], ca, na, p0 + r)
-                        add_t(tt[:, 1, r, :], cb, nb, p0 + r)
-                    tv = tt[:].rearrange("p s r c -> p (r c) s")
-                    cols = slice(p0 * P, (p0 + 2) * P)
-                    nc.scalar.activation(
-                        out=t2[:, cols, :], in_=tv, func=AF.Square, scale=(22.0**3 / 6.0) ** 0.5
-                    )
-                    nc.vector.tensor_tensor(out=t3[:, cols, :], in0=tv, in1=t2[:, cols, :], op=ALU.mult)
-            for q0 in range(0, rc, 4):
-                n = min(4, rc - q0)
-                uu = ps_u.tile([P, n, P], F32, name="uu")
-                for r in range(n):
+                uu = ps_u.tile([P, 4, P], F32, name="uu")
+                for r in range(4):
                     add_t(uu[:, r, :], q1, q2, q0 + r)
-                nc.scalar.activation(
-                    out=gd[:, q0 * P : (q0 + n) * P, :],
-                    in_=uu[:].rearrange("p r c -> p (r c)").unsqueeze(2).to_broadcast([P, n * P, 2]),
+                banks.append(uu)
+            return banks
+
+        def centre_steps(rc, banks):
+            gd = actp.tile([P, rc * P, 2], BF16, name="gd")
+            return gd, [
+                lambda b=b, uu=uu: nc.scalar.activation(
+                    out=gd[:, 4 * b * P : 4 * (b + 1) * P, :],
+                    in_=uu[:].rearrange("p r c -> p (r c)").unsqueeze(2).to_broadcast([P, 4 * P, 2]),
                     func=AF.Identity,
                     bias=g_bias[:, 0:1],
                     scale=g_scale[:, 0:1],
                 )
-            return t3, gd
+                for b, uu in enumerate(banks)
+            ]
 
-        def values(rc, tiles):
-            t3, gd = tiles
-            c = rc * P
-            pp = dvep.tile([P, 2, c, 2], BF16, name="pp")
+        def sides(rc, t3):
+            pp = dvep.tile([P, 2, rc * P, 2], BF16, name="pp")
             for s in range(2):
                 nc.vector.tensor_scalar(
                     out=pp[:, s, :, :], in0=t3[:], scalar1=1.0 - 2.0 * s, scalar2=0.0, op0=ALU.mult, op1=ALU.max
                 )
+            return pp
+
+        def join(rc, pp, gd):
+            c = rc * P
             g = dvep.tile([P, c, 2, 2], BF16, align_bytes=64, name="g")
             nc.vector.tensor_tensor(
                 out=g[:],
@@ -188,51 +241,135 @@ def tile_kan_layer_t_kernel(tc, x, spline_coeffs, out):
             )
             return g
 
-        def back(r0, rc, g, piece):
+        def quantise(rc, g, piece):
             codes = dvep.tile([P, rc * P], U32, align_bytes=64, name="codes")
             scales = dvep.tile([P, rc * P], U8, align_bytes=64, name="scales")
-            osb = outp.tile([P, rc, OUTS], F32, name="osb")
             gf = g[:].rearrange("p c s f -> p (c s f)")
-            for a in range(0, rc, piece):
-                b = a + piece
+            for a in range(0, rc * P, piece * P):
+                b = a + piece * P
                 nc.vector.quantize_mx(
-                    out=codes[:, a * P : b * P].bitcast(FP8X4),
-                    scales=scales[:, a * P : b * P],
-                    in_=gf[:, 4 * a * P : 4 * b * P],
+                    out=codes[:, a:b].bitcast(FP8X4), scales=scales[:, a:b], in_=gf[:, 4 * a : 4 * b]
                 )
-                for q0 in range(a, b, 4):
-                    n = min(4, b - q0)
-                    acc = ps_o.tile([P, n, OUTS], F32, name="acc")
-                    for j in range(n):
-                        c0 = (q0 + j) * P
-                        nc.tensor.matmul_mx(
-                            out=acc[:, j, :],
-                            lhsT=codes[:, c0 : c0 + P].bitcast(FP8X4),
-                            lhsT_scale=scales[:, c0 : c0 + P],
-                            rhs=w_codes[:].bitcast(FP8X4),
-                            rhs_scale=w_scales[:],
-                            start=True,
-                            stop=True,
-                        )
-                    nc.scalar.copy(out=osb[:, q0 : q0 + n, :], in_=acc[:])
-                nc.sync.dma_start(out=out_v[:, r0 + a : r0 + b, :], in_=osb[:, a:b, :])
+            return codes, scales
 
-        starts = []
-        r0 = 0
-        for rc in CHUNKS:
-            starts.append(r0)
-            r0 += rc
-        planes = folds(0, CHUNKS[0])
+        def product(rc, codes, scales):
+            banks = []
+            for q0 in range(0, rc, 4):
+                acc = ps_o.tile([P, 4, OUTS], F32, name="acc")
+                for j in range(4):
+                    c0 = (q0 + j) * P
+                    nc.tensor.matmul_mx(
+                        out=acc[:, j, :],
+                        lhsT=codes[:, c0 : c0 + P].bitcast(FP8X4),
+                        lhsT_scale=scales[:, c0 : c0 + P],
+                        rhs=w_codes[:].bitcast(FP8X4),
+                        rhs_scale=w_scales[:],
+                        start=True,
+                        stop=True,
+                    )
+                banks.append(acc)
+            return banks
+
+        def store_steps(r0, rc, banks, piece):
+            osb = outp.tile([P, rc, OUTS], F32, name="osb")
+
+            def step(b, acc):
+                nc.scalar.copy(out=osb[:, 4 * b : 4 * b + 4, :], in_=acc[:])
+                a, e = (4 * b, 4 * b + 4) if piece == 4 else (0, rc)
+                if e == 4 * b + 4:
+                    nc.sync.dma_start(out=out_v[:, r0 + a : r0 + e, :], in_=osb[:, a:e, :])
+
+            return [lambda b=b, acc=acc: step(b, acc) for b, acc in enumerate(banks)]
+
+        RC = CHUNKS[0]
+        count = len(CHUNKS)
+        sig, slopes, rising_a, rising_b, falling_a, falling_b, yhs, q1s, q2s = ({} for n in range(9))
+        dist, sq, centre, gds, t3s, prod = ({} for n in range(6))
+
+        def on_vector(n):
+            return n % 2 == 1
+
+        def rise_a(n):
+            rising_a[n] = clamp(RC, "ca", sig[n], ALU.max, 2.0 / 11, ALU.min, 6.0 / 11)
+
+        def rise_b(n):
+            rising_b[n] = clamp(RC, "cb", sig[n], ALU.max, 4.0 / 11, ALU.min, 8.0 / 11)
+
+        def fall(n):
+            m = slopes[n][:]
+            falling_a[n] = clamp(RC, "na", m, ALU.add, 1.0 / 11, ALU.max, -6.0 / 11)
+            if on_vector(n):
+                yhs[n] = fold_sum(RC, rising_b[n], slopes[n])
+            falling_b[n] = clamp(RC, "nb", m, ALU.max, -8.0 / 11, ALU.min, -4.0 / 11)
+
+        def fold_of(n):
+            if on_vector(n):
+                steps = fold_rest(yhs[n])
+            else:
+                yhs[n], steps = fold_steps(RC, sig[n])
+            q1s[n], more = square_steps(RC, yhs[n])
+            return steps + more
+
+        def weave(*lists):
+            for k in range(max(len(steps) for steps in lists)):
+                for steps in lists:
+                    if k < len(steps):
+                        steps[k]()
+
+        def start(n):
+            if n < count:
+                sig[n] = sigmoids(n * RC, RC)
+
+        def slope(n):
+            if n < count:
+                slopes[n] = half_slopes(RC, sig[n])
+
+        def fill(n):
+            dist[n] = distances(RC, *(flat(d[n]) for d in (rising_a, rising_b, falling_a, falling_b)))
+
+        start(0)
+        slope(0)
+        rise_a(0)
+        rise_b(0)
+        start(1)
+        fall(0)
+        slope(1)
+        rise_a(1)
+        fill(0)
+        weave(fold_of(0))
+        rise_b(1)
+        start(2)
         weights()
-        done = None
-        for n, rc in enumerate(CHUNKS):
-            mine = planes
-            if n + 1 < len(CHUNKS):
-                planes = folds(starts[n + 1], CHUNKS[n + 1])
-            tiles = cubes(rc, mine)
+        sq[0] = bank_squares(RC, dist[0])
+        fall(1)
+        q2s[0] = centre_cube(RC, yhs[0], q1s[0])
+        for n in range(count):
+            slope(n + 2)
+            centre[n] = centre_sums(RC, *(d[n][:].rearrange("p r h f -> p (r h f)") for d in (q1s, q2s)))
+            t3s[n] = cubes(RC, dist[n], sq[n])
+            gds[n], steps = centre_steps(RC, centre[n])
+            out_steps = store_steps((n - 2) * RC, RC, prod[n - 2], RC) if n > 1 else []
+            weave(fold_of(n + 1) if n + 1 < count else [], out_steps + steps)
             if n:
-                g = values(CHUNKS[n - 1], done)
-                back(starts[n - 1], CHUNKS[n - 1], g, CHUNKS[n - 1])
-            done = tiles
-        g = values(CHUNKS[-1], done)
-        back(starts[-1], CHUNKS[-1], g, 2)
+                pp = sides(RC, t3s[n - 1])
+            if n + 1 < count:
+                fill(n + 1)
+            if n + 2 < count:
+                rise_a(n + 2)
+            start(n + 3)
+            if n + 1 < count:
+                sq[n + 1] = bank_squares(RC, dist[n + 1])
+            if n:
+                g = join(RC, pp, gds[n - 1])
+            if n + 1 < count:
+                q2s[n + 1] = centre_cube(RC, yhs[n + 1], q1s[n + 1])
+            if n:
+                prod[n - 1] = product(RC, *quantise(RC, g, RC))
+            if n + 2 < count:
+                rise_b(n + 2)
+                fall(n + 2)
+        pp = sides(RC, t3s[count - 1])
+        weave(store_steps((count - 2) * RC, RC, prod[count - 2], RC))
+        g = join(RC, pp, gds[count - 1])
+        prod[count - 1] = product(RC, *quantise(RC, g, 4))
+        weave(store_steps((count - 1) * RC, RC, prod[count - 1], 4))

@@ -41,10 +41,9 @@ def tile_kan_layer_t_kernel(tc, x, spline_coeffs, out):
 
         x_sb = const.tile([P, ROWS, FEAT], BF16)
         w_sb = const.tile([P, FEAT * 8], BF16)
-        for n, (a, b) in enumerate(LOADS):
+        nc.scalar.dma_start(out=w_sb[:], in_=spline_coeffs.rearrange("o i k -> o (i k)"))
+        for a, b in LOADS:
             nc.sync.dma_start(out=x_sb[:, a:b, :], in_=x_v[:, a:b, :])
-            if n == 0:
-                nc.sync.dma_start(out=w_sb[:], in_=spline_coeffs.rearrange("o i k -> o (i k)"))
 
         ident = const.tile([P, P], F32)
         make_identity(nc, ident[:])
@@ -91,6 +90,9 @@ def tile_kan_layer_t_kernel(tc, x, spline_coeffs, out):
             w_t = ps_o.tile([P, 4, OUTS], BF16, name="acc")
             for t in range(4):
                 nc.tensor.transpose(w_t[:, t, :], wg[:, t, :, :].rearrange("o h f -> o (h f)"), ident_b[:])
+            return w_t
+
+        def weight_codes(w_t):
             wq = const.tile([P, OUTS, 4], BF16, align_bytes=64)
             nc.vector.tensor_copy(out=wq[:], in_=w_t[:].rearrange("p t o -> p o t"))
             nc.vector.quantize_mx(
@@ -222,23 +224,36 @@ def tile_kan_layer_t_kernel(tc, x, spline_coeffs, out):
                 for b, uu in enumerate(banks)
             ]
 
-        def sides(rc, t3):
+        def sides(rc, t3, pieces=1, share=False):
             pp = dvep.tile([P, 2, rc * P, 2], BF16, name="pp")
-            for s in range(2):
-                nc.vector.tensor_scalar(
-                    out=pp[:, s, :, :], in0=t3[:], scalar1=1.0 - 2.0 * s, scalar2=0.0, op0=ALU.mult, op1=ALU.max
-                )
+            c = rc * P // pieces
+            for a in range(0, rc * P, c):
+                for s in range(2):
+                    if s and share:
+                        nc.scalar.activation(
+                            out=pp[:, s, a : a + c, :], in_=t3[:, a : a + c, :], func=AF.Relu, scale=-1.0
+                        )
+                        continue
+                    nc.vector.tensor_scalar(
+                        out=pp[:, s, a : a + c, :],
+                        in0=t3[:, a : a + c, :],
+                        scalar1=1.0 - 2.0 * s,
+                        scalar2=0.0,
+                        op0=ALU.mult,
+                        op1=ALU.max,
+                    )
             return pp
 
-        def join(rc, pp, gd):
-            c = rc * P
-            g = dvep.tile([P, c, 2, 2], BF16, align_bytes=64, name="g")
-            nc.vector.tensor_tensor(
-                out=g[:],
-                in0=pp[:].rearrange("p s c f -> p c s f"),
-                in1=gd[:].unsqueeze(2).to_broadcast([P, c, 2, 2]),
-                op=ALU.min,
-            )
+        def join(rc, pp, gd, pieces=1):
+            g = dvep.tile([P, rc * P, 2, 2], BF16, align_bytes=64, name="g")
+            c = rc * P // pieces
+            for a in range(0, rc * P, c):
+                nc.vector.tensor_tensor(
+                    out=g[:, a : a + c, :, :],
+                    in0=pp[:, :, a : a + c, :].rearrange("p s c f -> p c s f"),
+                    in1=gd[:, a : a + c, :].unsqueeze(2).to_broadcast([P, c, 2, 2]),
+                    op=ALU.min,
+                )
             return g
 
         def quantise(rc, g, piece):
@@ -287,7 +302,7 @@ def tile_kan_layer_t_kernel(tc, x, spline_coeffs, out):
         dist, sq, centre, gds, t3s, prod = ({} for n in range(6))
 
         def on_vector(n):
-            return n % 2 == 1
+            return n % 4 == 1 and n < 12
 
         def rise_a(n):
             rising_a[n] = clamp(RC, "ca", sig[n], ALU.max, 2.0 / 11, ALU.min, 6.0 / 11)
@@ -327,6 +342,7 @@ def tile_kan_layer_t_kernel(tc, x, spline_coeffs, out):
         def fill(n):
             dist[n] = distances(RC, *(flat(d[n]) for d in (rising_a, rising_b, falling_a, falling_b)))
 
+        w_t = weights()
         start(0)
         slope(0)
         rise_a(0)
@@ -339,7 +355,7 @@ def tile_kan_layer_t_kernel(tc, x, spline_coeffs, out):
         weave(fold_of(0))
         rise_b(1)
         start(2)
-        weights()
+        weight_codes(w_t)
         sq[0] = bank_squares(RC, dist[0])
         fall(1)
         q2s[0] = centre_cube(RC, yhs[0], q1s[0])
@@ -368,8 +384,8 @@ def tile_kan_layer_t_kernel(tc, x, spline_coeffs, out):
             if n + 2 < count:
                 rise_b(n + 2)
                 fall(n + 2)
-        pp = sides(RC, t3s[count - 1])
+        pp = sides(RC, t3s[count - 1], 2, True)
         weave(store_steps((count - 2) * RC, RC, prod[count - 2], RC))
-        g = join(RC, pp, gds[count - 1])
+        g = join(RC, pp, gds[count - 1], 2)
         prod[count - 1] = product(RC, *quantise(RC, g, 4))
         weave(store_steps((count - 1) * RC, RC, prod[count - 1], 4))

from contextlib import ExitStack

import concourse.mybir as mybir
from concourse.masks import make_identity

FLOPS = 2 * 16384 * 512 * 128

F32 = mybir.dt.float32
BF16 = mybir.dt.bfloat16
U32 = mybir.dt.uint32
U8 = mybir.dt.uint8
FP8X4 = mybir.dt.float8_e4m3fn_x4
ALU = mybir.AluOpType
AF = mybir.ActivationFunctionType

P = 128
ROWS = 128
FEAT = 64
OUTS = 128
CHUNKS = (8,) * 16
LOADS = ((0, 8), (8, 16), (16, 32), (32, 64), (64, 128))
SLOT_K = (4, 6, 0, 2)
assert sum(CHUNKS) == ROWS


def tile_kan_layer_t_kernel(tc, x, spline_coeffs, out):
    nc = tc.nc
    x_v = x.rearrange("(p r) i -> p r i", r=ROWS)
    out_v = out.rearrange("(p r) o -> p r o", r=ROWS)
    with ExitStack() as ctx:
        const = ctx.enter_context(tc.tile_pool(name="const", bufs=1))
        fold = ctx.enter_context(tc.tile_pool(name="fold", bufs=2))
        sgp = ctx.enter_context(tc.tile_pool(name="sgp", bufs=3))
        half_slope = ctx.enter_context(tc.tile_pool(name="half_slope", bufs=1))
        actp = ctx.enter_context(tc.tile_pool(name="actp", bufs=3))
        dvep = ctx.enter_context(tc.tile_pool(name="dvep", bufs=3))
        outp = ctx.enter_context(tc.tile_pool(name="outp", bufs=3))
        ps_t = ctx.enter_context(tc.psum_pool(name="ps_t", bufs=4))
        ps_u = ctx.enter_context(tc.psum_pool(name="ps_u", bufs=2))
        ps_o = ctx.enter_context(tc.psum_pool(name="ps_o", bufs=2))

        x_sb = const.tile([P, ROWS, FEAT], BF16)
        w_sb = const.tile([P, FEAT * 8], BF16)
        nc.scalar.dma_start(out=w_sb[:], in_=spline_coeffs.rearrange("o i k -> o (i k)"))
        for a, b in LOADS:
            nc.sync.dma_start(out=x_sb[:, a:b, :], in_=x_v[:, a:b, :])

        ident = const.tile([P, P], F32)
        make_identity(nc, ident[:])
        ident_b = const.tile([P, P], BF16)
        nc.vector.tensor_copy(out=ident_b[:], in_=ident[:])
        one = const.tile([P, 1], F32)
        nc.vector.memset(one[:], 1.0)
        half_neg = const.tile([P, 1], F32)
        nc.vector.memset(half_neg[:], -0.5)
        fold_bias = []
        for n, value in enumerate((-6.0, -4.0, -2.0)):
            bias_t = const.tile([P, 1], F32, name="fold_bias%d" % n)
            nc.vector.memset(bias_t[:], value)
            fold_bias.append(bias_t)
        three_halves = const.tile([P, 1], F32)
        nc.vector.memset(three_halves[:], 1.5)
        root2 = const.tile([P, 1], F32)
        nc.vector.tensor_scalar(out=root2[:], in0=one[:], scalar1=2.0**0.5, scalar2=None, op0=ALU.mult)
        par = const.tile([P, 1], F32)
        nc.vector.tensor_reduce(
            out=par[:],
            in_=ident[:, FEAT:P],
            axis=mybir.AxisListType.X,
            op=ALU.add,
        )
        g_scale = const.tile([P, 1], F32)
        nc.vector.tensor_scalar(out=g_scale[:], in0=par[:], scalar1=1.0, scalar2=-0.5, op0=ALU.mult, op1=ALU.add)
        g_bias = const.tile([P, 1], F32)
        nc.vector.tensor_scalar(
            out=g_bias[:], in0=par[:], scalar1=1.0 / 24 - 2.0 / 3, scalar2=2.0 / 3, op0=ALU.mult, op1=ALU.add
        )

        w_codes = const.tile([P, OUTS], U32, align_bytes=64)
        w_scales = const.tile([P, OUTS], U8, align_bytes=64)

        def weights():
            w4 = w_sb[:].rearrange("o (u l j k) -> o l u j k", l=4, j=4, k=8)
            wg = const.tile([P, 4, 2, FEAT], BF16)
            for t in range(4):
                for h, k in enumerate((SLOT_K[t], 7 - SLOT_K[t])):
                    nc.vector.tensor_copy(
                        out=wg[:, t, h, :].rearrange("o (l u j) -> o l u j", l=4, j=4), in_=w4[:, :, :, :, k]
                    )
            w_t = ps_o.tile([P, 4, OUTS], BF16, name="acc")
            for t in range(4):
                nc.tensor.transpose(w_t[:, t, :], wg[:, t, :, :].rearrange("o h f -> o (h f)"), ident_b[:])
            return w_t

        def weight_codes(w_t):
            wq = const.tile([P, OUTS, 4], BF16, align_bytes=64)
            nc.vector.tensor_copy(out=wq[:], in_=w_t[:].rearrange("p t o -> p o t"))
            nc.vector.quantize_mx(
                out=w_codes[:].bitcast(FP8X4), scales=w_scales[:], in_=wq[:].rearrange("p o t -> p (o t)")
            )

        def sigmoids(r0, rc):
            sg = sgp.tile([P, 2, 4, rc * 4, 4], F32, name="sg")
            xin = x_sb[:, r0 : r0 + rc, :].rearrange("p r (u l j) -> p l (r u) j", l=4, j=4)
            for h in range(2):
                nc.scalar.activation(out=sg[:, h, :, :, :], in_=xin, func=AF.Sigmoid, scale=2.0 - 4.0 * h)
            return sg[:].rearrange("p h l (r u) j -> p r (h l) (u j)", u=4)

        def half_slopes(rc, s):
            m_t = half_slope.tile([P, rc, 8, 16], F32, name="m_t")
            nc.gpsimd.tensor_scalar(
                out=m_t[:], in0=s, scalar1=-0.5, scalar2=-3.0 / 11, op0=ALU.mult, op1=ALU.add
            )
            return m_t

        def clamp(rc, name, src, op0, scalar1, op1, scalar2):
            t = fold.tile([P, rc, 8, 16], F32, name=name)
            nc.vector.tensor_scalar(out=t[:], in0=src, scalar1=scalar1, scalar2=scalar2, op0=op0, op1=op1)
            return t

        def flat(t):
            return t[:].rearrange("p r k f -> p (r k f)")

        def fold_steps(rc, s):
            ee = fold.tile([P, rc, FEAT], F32, name="ee")
            biases = fold_bias + [half_neg]
            steps = [
                lambda: nc.scalar.activation(
                    out=ee[:].rearrange("p r (l f) -> p r l f", l=4),
                    in_=s[:, :, 0:4, :],
                    func=AF.Abs,
                    bias=biases[0][:, 0:1],
                    scale=11.0,
                )
            ]
            for n in range(1, 4):
                steps.append(
                    lambda n=n: nc.scalar.activation(
                        out=ee[:], in_=ee[:], func=AF.Abs, bias=biases[n][:, 0:1], scale=(1.0, 0.5)[n // 3]
                    )
                )
            return ee, steps

        def fold_sum(rc, cb, m):
            ee = fold.tile([P, rc, FEAT], F32, name="ee")
            even = [flat(t).rearrange("p (r h f) -> p r h f", h=2, f=FEAT)[:, :, 0, :] for t in (cb, m)]
            nc.vector.tensor_tensor(out=ee[:], in0=even[0], in1=even[1], op=ALU.add)
            return ee

        def fold_rest(ee):
            return [
                lambda: nc.scalar.activation(out=ee[:], in_=ee[:], func=AF.Abs, scale=22.0),
                lambda: nc.scalar.activation(out=ee[:], in_=ee[:], func=AF.Abs, bias=half_neg[:, 0:1], scale=0.5),
            ]

        def square_steps(rc, yh):
            q1 = fold.tile([P, rc, 2, FEAT], F32, name="q1")
            return q1, [
                lambda: nc.scalar.activation(
                    out=q1[:, :, 0, :], in_=yh[:], func=AF.Square, bias=root2[:, 0:1], scale=-2.0 * 2.0**0.5
                ),
                lambda: nc.scalar.activation(
                    out=q1[:, :, 1, :], in_=yh[:], func=AF.Square, bias=three_halves[:, 0:1], scale=-2.0
                ),
            ]

        def centre_cube(rc, yh, q1):
            q2 = fold.tile([P, rc, 2, FEAT], F32, name="q2")
            nc.vector.scalar_tensor_tensor(
                out=q2[:, :, 0, :], in0=yh[:], scalar=0.5, in1=q1[:, :, 0, :], op0=ALU.subtract, op1=ALU.mult
            )
            nc.sync.dma_start(out=q2[:, :, 1, :], in_=q2[:, :, 0, :])
            return q2

        def add_t(dst, one_plane, other_plane, r):
            for n, plane in enumerate((one_plane, other_plane)):
                nc.tensor.matmul(
                    dst, lhsT=plane[:, r * P : (r + 1) * P], rhs=ident[:], start=n == 0, stop=n == 1, is_transpose=True
                )

        def distances(rc, ca, cb, na, nb):
            banks = []
            for p0 in range(0, rc, 2):
                tt = ps_t.tile([P, 2, 2, P], F32, name="tt")
                for r in range(2):
                    add_t(tt[:, 0, r, :], ca, na, p0 + r)
                    add_t(tt[:, 1, r, :], cb, nb, p0 + r)
                banks.append(tt[:].rearrange("p s r c -> p (r c) s"))
            return banks

        def bank_squares(rc, banks):
            t2 = actp.tile([P, rc * P, 2], F32, name="t2")
            for b, tv in enumerate(banks):
                cols = slice(2 * b * P, (2 * b + 2) * P)
                nc.scalar.activation(out=t2[:, cols, :], in_=tv, func=AF.Square, scale=(22.0**3 / 6.0) ** 0.5)
            return t2

        def cubes(rc, banks, t2):
            t3 = dvep.tile([P, rc * P, 2], BF16, name="t3")
            for b, tv in enumerate(banks):
                cols = slice(2 * b * P, (2 * b + 2) * P)
                nc.vector.tensor_tensor(out=t3[:, cols, :], in0=tv, in1=t2[:, cols, :], op=ALU.mult)
            return t3

        def centre_sums(rc, q1, q2):
            banks = []
            for q0 in range(0, rc, 4):
                uu = ps_u.tile([P, 4, P], F32, name="uu")
                for r in range(4):
                    add_t(uu[:, r, :], q1, q2, q0 + r)
                banks.append(uu)
            return banks

        def centre_steps(rc, banks):
            gd = actp.tile([P, rc * P, 2], BF16, name="gd")
            return gd, [
                lambda b=b, uu=uu: nc.scalar.activation(
                    out=gd[:, 4 * b * P : 4 * (b + 1) * P, :],
                    in_=uu[:].rearrange("p r c -> p (r c)").unsqueeze(2).to_broadcast([P, 4 * P, 2]),
                    func=AF.Identity,
                    bias=g_bias[:, 0:1],
                    scale=g_scale[:, 0:1],
                )
                for b, uu in enumerate(banks)
            ]

        def sides(rc, t3, pieces=1, share=False):
            pp = dvep.tile([P, 2, rc * P, 2], BF16, name="pp")
            c = rc * P // pieces
            for a in range(0, rc * P, c):
                for s in range(2):
                    if s and share:
                        nc.scalar.activation(
                            out=pp[:, s, a : a + c, :], in_=t3[:, a : a + c, :], func=AF.Relu, scale=-1.0
                        )
                        continue
                    nc.vector.tensor_scalar(
                        out=pp[:, s, a : a + c, :],
                        in0=t3[:, a : a + c, :],
                        scalar1=1.0 - 2.0 * s,
                        scalar2=0.0,
                        op0=ALU.mult,
                        op1=ALU.max,
                    )
            return pp

        def join(rc, pp, gd, pieces=1):
            g = dvep.tile([P, rc * P, 2, 2], BF16, align_bytes=64, name="g")
            c = rc * P // pieces
            for a in range(0, rc * P, c):
                nc.vector.tensor_tensor(
                    out=g[:, a : a + c, :, :],
                    in0=pp[:, :, a : a + c, :].rearrange("p s c f -> p c s f"),
                    in1=gd[:, a : a + c, :].unsqueeze(2).to_broadcast([P, c, 2, 2]),
                    op=ALU.min,
                )
            return g

        def quantise(rc, g, piece):
            codes = dvep.tile([P, rc * P], U32, align_bytes=64, name="codes")
            scales = dvep.tile([P, rc * P], U8, align_bytes=64, name="scales")
            gf = g[:].rearrange("p c s f -> p (c s f)")
            for a in range(0, rc * P, piece * P):
                b = a + piece * P
                nc.vector.quantize_mx(
                    out=codes[:, a:b].bitcast(FP8X4), scales=scales[:, a:b], in_=gf[:, 4 * a : 4 * b]
                )
            return codes, scales

        def product(rc, codes, scales):
            banks = []
            for q0 in range(0, rc, 4):
                acc = ps_o.tile([P, 4, OUTS], F32, name="acc")
                for j in range(4):
                    c0 = (q0 + j) * P
                    nc.tensor.matmul_mx(
                        out=acc[:, j, :],
                        lhsT=codes[:, c0 : c0 + P].bitcast(FP8X4),
                        lhsT_scale=scales[:, c0 : c0 + P],
                        rhs=w_codes[:].bitcast(FP8X4),
                        rhs_scale=w_scales[:],
                        start=True,
                        stop=True,
                    )
                banks.append(acc)
            return banks

        def store_steps(r0, rc, banks, piece):
            osb = outp.tile([P, rc, OUTS], F32, name="osb")

            def step(b, acc):
                nc.scalar.copy(out=osb[:, 4 * b : 4 * b + 4, :], in_=acc[:])
                a, e = (4 * b, 4 * b + 4) if piece == 4 else (0, rc)
                if e == 4 * b + 4:
                    nc.sync.dma_start(out=out_v[:, r0 + a : r0 + e, :], in_=osb[:, a:e, :])

            return [lambda b=b, acc=acc: step(b, acc) for b, acc in enumerate(banks)]

        RC = CHUNKS[0]
        count = len(CHUNKS)
        sig, slopes, rising_a, rising_b, falling_a, falling_b, yhs, q1s, q2s = ({} for n in range(9))
        dist, sq, centre, gds, t3s, prod = ({} for n in range(6))

        def on_vector(n):
            return n % 4 == 1 and n < 12

        def rise_a(n):
            rising_a[n] = clamp(RC, "ca", sig[n], ALU.max, 2.0 / 11, ALU.min, 6.0 / 11)

        def rise_b(n):
            rising_b[n] = clamp(RC, "cb", sig[n], ALU.max, 4.0 / 11, ALU.min, 8.0 / 11)

        def fall(n):
            m = slopes[n][:]
            falling_a[n] = clamp(RC, "na", m, ALU.add, 1.0 / 11, ALU.max, -6.0 / 11)
            if on_vector(n):
                yhs[n] = fold_sum(RC, rising_b[n], slopes[n])
            falling_b[n] = clamp(RC, "nb", m, ALU.max, -8.0 / 11, ALU.min, -4.0 / 11)

        def fold_of(n):
            if on_vector(n):
                steps = fold_rest(yhs[n])
            else:
                yhs[n], steps = fold_steps(RC, sig[n])
            q1s[n], more = square_steps(RC, yhs[n])
            return steps + more

        def weave(*lists):
            for k in range(max(len(steps) for steps in lists)):
                for steps in lists:
                    if k < len(steps):
                        steps[k]()

        def start(n):
            if n < count:
                sig[n] = sigmoids(n * RC, RC)

        def slope(n):
            if n < count:
                slopes[n] = half_slopes(RC, sig[n])

        def fill(n):
            dist[n] = distances(RC, *(flat(d[n]) for d in (rising_a, rising_b, falling_a, falling_b)))

        w_t = weights()
        start(0)
        slope(0)
        rise_a(0)
        rise_b(0)
        start(1)
        fall(0)
        slope(1)
        rise_a(1)
        fill(0)
        weave(fold_of(0))
        rise_b(1)
        start(2)
        weight_codes(w_t)
        sq[0] = bank_squares(RC, dist[0])
        fall(1)
        q2s[0] = centre_cube(RC, yhs[0], q1s[0])
        for n in range(count):
            slope(n + 2)
            centre[n] = centre_sums(RC, *(d[n][:].rearrange("p r h f -> p (r h f)") for d in (q1s, q2s)))
            t3s[n] = cubes(RC, dist[n], sq[n])
            gds[n], steps = centre_steps(RC, centre[n])
            out_steps = store_steps((n - 2) * RC, RC, prod[n - 2], RC) if n > 1 else []
            weave(fold_of(n + 1) if n + 1 < count else [], out_steps + steps)
            if n:
                pp = sides(RC, t3s[n - 1])
            if n + 1 < count:
                fill(n + 1)
            if n + 2 < count:
                rise_a(n + 2)
            start(n + 3)
            if n + 1 < count:
                sq[n + 1] = bank_squares(RC, dist[n + 1])
            if n:
                g = join(RC, pp, gds[n - 1])
            if n + 1 < count:
                q2s[n + 1] = centre_cube(RC, yhs[n + 1], q1s[n + 1])
            if n:
                prod[n - 1] = product(RC, *quantise(RC, g, RC))
            if n + 2 < count:
                rise_b(n + 2)
                fall(n + 2)
        pp = sides(RC, t3s[count - 1], 2, True)
        weave(store_steps((count - 2) * RC, RC, prod[count - 2], RC))
        g = join(RC, pp, gds[count - 1], 2)
        prod[count - 1] = product(RC, *quantise(RC, g, 4))
        weave(store_steps((count - 1) * RC, RC, prod[count - 1], 4))
